import numpy as np
import ml_dtypes


def mxq(x, axis, fmt="e4m3"):
    dtype, down = {"e4m3": (ml_dtypes.float8_e4m3fn, 7), "e5m2": (ml_dtypes.float8_e5m2, 14)}[fmt]
    v = np.moveaxis(np.asarray(x, np.float32).astype(ml_dtypes.bfloat16).astype(np.float64), axis, -1)
    blocks = v.reshape(v.shape[:-1] + (-1, 32))
    amax = np.abs(blocks).max(-1, keepdims=True)
    byte = np.maximum(np.where(amax > 0, np.frexp(amax)[1] - 1 + 127, 0) - down, 1)
    scale = np.exp2(byte - 127.0)
    codes = (blocks / scale).astype(np.float32).astype(dtype).astype(np.float64)
    return np.moveaxis((codes * scale).reshape(v.shape), -1, axis)


WIDE = False


def mx_kscale(k):
    if not WIDE:
        return np.ones(k)
    levels = np.array([10, -10, 5, -5, 0])
    a = np.random.permutation(np.resize(levels, k // 512 * 4)).reshape(k // 512, 4)
    idx = np.arange(k)
    return np.exp2(a[idx // 512, idx % 128 // 32])


BF16 = ml_dtypes.bfloat16


def bf(x):
    return np.asarray(x, np.float32).astype(BF16)


def f64(x):
    return np.asarray(x).astype(np.float64)


B, I, H = 4096, 512, 512
DT = 0.1


def sigmoid(v):
    return 1.0 / (1.0 + np.exp(-v))


def setup_inputs():
    s = mx_kscale(I)
    wt = np.random.standard_normal((H, I + H)) * 1.5 / np.sqrt(I + H)
    wt[:, :I] = wt[:, :I] / s
    return {"x": bf(np.random.standard_normal((B, I)) * s),
            "hidden": bf(np.random.standard_normal((B, H))),
            "W_rec": bf(np.random.standard_normal((H, H)) * 1.0 / np.sqrt(H)),
            "W_in_w": bf(np.random.standard_normal((H, I)) * 0.8 / np.sqrt(I) / s),
            "W_in_b": bf(np.random.standard_normal(H) * 0.5),
            "tau_base": bf(0.3 + 0.3 * np.random.random(H)),
            "tau_adapt_w": bf(wt),
            "tau_adapt_b": bf(np.random.standard_normal(H) * 0.5)}


def reference(x, hidden, W_rec, W_in_w, W_in_b, tau_base, tau_adapt_w, tau_adapt_b):
    h = f64(hidden)
    wt = f64(tau_adapt_w)
    xq = mxq(f64(x), 1, "e4m3")
    hq = mxq(h, 1, "e4m3")
    input_contrib = (xq @ mxq(f64(W_in_w), 1, "e4m3").T) + f64(W_in_b)
    x_tau = xq @ mxq(wt[:, :I], 1, "e4m3").T
    tau_logits = x_tau + (hq @ mxq(wt[:, I:], 1, "e4m3").T) + f64(tau_adapt_b)
    tau = f64(tau_base) * (0.5 + sigmoid(tau_logits))
    activated = np.tanh((hq @ mxq(f64(W_rec), 1, "e4m3").T) + input_contrib)
    return h + DT * (-h + activated) / tau

@@ -1,0 +1,235 @@
+from contextlib import ExitStack
+import math
+
+import concourse.masks as masks
+import concourse.mybir as mybir
+
+F32 = mybir.dt.float32
+BF16 = mybir.dt.bfloat16
+U32 = mybir.dt.uint32
+U8 = mybir.dt.uint8
+FP8X4 = mybir.dt.float8_e4m3fn_x4
+ALU = mybir.AluOpType
+ACT = mybir.ActivationFunctionType
+
+P = 128
+B, I, H = 4096, 512, 512
+CHUNK = 512
+N_CHUNKS = B // CHUNK
+FLOPS = 4 * 2 * B * 512 * 512
+
+
+def tile_liquidcell_pa_t_kernel(
+    tc, x, hidden, W_rec, W_in_w, W_in_b, tau_base, tau_adapt_w, tau_adapt_b, out
+):
+    nc = tc.nc
+    with ExitStack() as ctx:
+        const = ctx.enter_context(tc.tile_pool(name="const", bufs=1))
+        nat = ctx.enter_context(tc.tile_pool(name="nat", bufs=1))
+        wq = ctx.enter_context(tc.tile_pool(name="wq", bufs=1))
+        grp = ctx.enter_context(tc.tile_pool(name="grp", bufs=2))
+        qp = ctx.enter_context(tc.tile_pool(name="qp", bufs=2))
+        ep = ctx.enter_context(tc.tile_pool(name="ep", bufs=2))
+        tp_psum = ctx.enter_context(tc.psum_pool(name="tp_psum", bufs=2))
+        acc_psum = ctx.enter_context(tc.psum_pool(name="acc_psum", bufs=4))
+        bt_psum = ctx.enter_context(tc.psum_pool(name="bt_psum", bufs=2))
+
+        warm = const.tile([P, 1], F32, name="warm")
+        nc.vector.memset(warm[:], 0.0)
+        warm2 = const.tile([P, 1], F32, name="warm2")
+        nc.scalar.activation(out=warm2[:], in_=warm[:], func=ACT.Tanh)
+
+        ident = const.tile([P, P], F32, name="ident")
+        masks.make_identity(nc, ident[:])
+
+        vec_rows = const.tile([P, 256], BF16, name="vec_rows")
+        nc.vector.memset(vec_rows[:], 0.0)
+        for i, vec in enumerate((W_in_b, tau_base, tau_adapt_b)):
+            nc.scalar.dma_start(
+                out=vec_rows[2 * i : 2 * i + 2, :],
+                in_=vec.rearrange("(u w) -> u w", u=2),
+            )
+
+        win_nat = nat.tile([P, 4, 512], BF16, name="win_nat")
+        wrec_nat = nat.tile([P, 4, 512], BF16, name="wrec_nat")
+        wtau_nat = nat.tile([P, 4, 1024], BF16, name="wtau_nat")
+        x_nat = []
+        h_nat = []
+        for c in range(N_CHUNKS):
+            x_nat.append(nat.tile([P, 4, 512], BF16, name="x_nat%d" % c))
+            h_nat.append(nat.tile([P, 4, 512], BF16, name="h_nat%d" % c))
+
+        def load_weight(dst, src):
+            nc.sync.dma_start(
+                out=dst[:].rearrange("p (u e) k -> p u e k", u=2),
+                in_=src.rearrange("(u p e) k -> p u e k", u=2, e=2),
+            )
+
+        def load_chunk(c):
+            rows = slice(c * CHUNK, (c + 1) * CHUNK)
+            nc.sync.dma_start(
+                out=x_nat[c][:], in_=x[rows, :].rearrange("(p r) k -> p r k", r=4)
+            )
+            nc.sync.dma_start(
+                out=h_nat[c][:], in_=hidden[rows, :].rearrange("(p r) k -> p r k", r=4)
+            )
+
+        load_weight(win_nat, W_in_w)
+        load_weight(wrec_nat, W_rec)
+        load_chunk(0)
+        load_weight(wtau_nat, tau_adapt_w)
+        for c in range(1, N_CHUNKS):
+            load_chunk(c)
+
+        def copy_on(engine, dst, src):
+            if engine == "v":
+                nc.vector.tensor_copy(out=dst, in_=src)
+            else:
+                nc.scalar.copy(out=dst, in_=src)
+
+        def transpose_group(src_words, grouped, engines):
+            gw = grouped[:].bitcast(F32).rearrange("p (b u) -> p b u", u=2)
+            for half in range(2):
+                bank = tp_psum.tile([P, 2, 256], F32, name="bank", tag="tp")
+                for j in range(2):
+                    r = 2 * half + j
+                    for u in range(2):
+                        nc.tensor.transpose(
+                            bank[:, u, j * P : (j + 1) * P],
+                            src_words[:, r, u * P : (u + 1) * P],
+                            ident[:],
+                        )
+                copy_on(
+                    engines[half],
+                    gw[:, half * 256 : (half + 1) * 256, :],
+                    bank[:].rearrange("p u b -> p b u"),
+                )
+
+        def quantise(grouped, codes, scales):
+            nc.vector.quantize_mx(
+                out=codes[:].bitcast(FP8X4), scales=scales[:], in_=grouped[:]
+            )
+
+        w_codes = {}
+        w_scales = {}
+
+        def prep_weight(o, g, src_words, engines):
+            gwt = grp.tile([P, 2048], BF16, name="gwt", tag="gw", align_bytes=64)
+            transpose_group(src_words, gwt, engines)
+            w_codes[(o, g)] = wq.tile(
+                [P, 512], U32, name="w_codes%d%d" % (o, g), align_bytes=64
+            )
+            w_scales[(o, g)] = wq.tile(
+                [P, 512], U8, name="w_scales%d%d" % (o, g), align_bytes=64
+            )
+            quantise(gwt, w_codes[(o, g)], w_scales[(o, g)])
+
+        act = {}
+
+        def forward(c):
+            gx = grp.tile([P, 2048], BF16, name="gx", tag="gx", align_bytes=64)
+            gh = grp.tile([P, 2048], BF16, name="gh", tag="gh", bufs=3, align_bytes=64)
+            transpose_group(x_nat[c][:].bitcast(F32), gx, ("v", "s"))
+            transpose_group(h_nat[c][:].bitcast(F32), gh, ("s", "s"))
+            xc = qp.tile([P, 512], U32, name="xc", tag="xc", align_bytes=64)
+            xs = qp.tile([P, 512], U8, name="xs", tag="xs", align_bytes=64)
+            hc = qp.tile([P, 512], U32, name="hc", tag="hc", align_bytes=64)
+            hs = qp.tile([P, 512], U8, name="hs", tag="hs", align_bytes=64)
+            quantise(gx, xc, xs)
+            quantise(gh, hc, hs)
+            act[c] = (gh, ((xc, xs), (hc, hs)))
+
+        prep_weight(0, 0, win_nat[:].bitcast(F32), ("v", "s"))
+        prep_weight(0, 1, wrec_nat[:].bitcast(F32), ("v", "s"))
+        forward(0)
+        wtau_words = wtau_nat[:].bitcast(F32)
+        prep_weight(1, 0, wtau_words[:, :, 0:256], ("v", "s"))
+        prep_weight(1, 1, wtau_words[:, :, 256:512], ("v", "s"))
+
+        vt = tp_psum.tile([P, 2, 256], F32, name="vt", tag="tp")
+        nc.tensor.transpose(vt[:, 0, 0:P], vec_rows[:].bitcast(F32), ident[:])
+        cst = const.tile([P, 12], F32, name="cst")
+        nc.vector.tensor_copy(
+            out=cst[:], in_=vt[:].rearrange("p u b -> p (u b)").bitcast(BF16)[:, 0:12]
+        )
+        b_tau = const.tile([P, 4], F32, name="b_tau")
+        nc.vector.tensor_scalar(
+            out=b_tau[:], in0=cst[:, 8:12], scalar1=0.5, scalar2=0.5 * math.log(3.0),
+            op0=ALU.mult, op1=ALU.add,
+        )
+        inv_tb = const.tile([P, 4], F32, name="inv_tb")
+        nc.vector.reciprocal(out=inv_tb[:], in_=cst[:, 4:8])
+        neg_c = const.tile([P, 4], F32, name="neg_c")
+        nc.vector.tensor_scalar_mul(out=neg_c[:], in0=inv_tb[:], scalar1=-1.0 / 15.0)
+
+        res = {}
+
+        def matmuls(c):
+            gh, ops = act[c]
+            a_t = ep.tile([P, 4, 512], F32, name="a_t", tag="a_t", bufs=3)
+            v_t = ep.tile([P, 4, 512], F32, name="v_t", tag="v_t")
+            h_T = gh[:].rearrange("p (b t) -> p t b", t=4)
+            for o in range(2):
+                for t in range(4):
+                    acc = acc_psum.tile([P, 512], F32, name="acc", tag="acc")
+                    cols = slice(t * P, (t + 1) * P)
+                    for g in range(2):
+                        nc.tensor.matmul_mx(
+                            out=acc[:],
+                            lhsT=w_codes[(o, g)][:, cols].bitcast(FP8X4),
+                            lhsT_scale=w_scales[(o, g)][:, cols],
+                            rhs=ops[g][0][:].bitcast(FP8X4),
+                            rhs_scale=ops[g][1][:],
+                            start=(g == 0),
+                            stop=(g == 1),
+                        )
+                    if o == 0:
+                        nc.scalar.activation(
+                            out=a_t[:, t, :], in_=acc[:], func=ACT.Tanh,
+                            bias=cst[:, t : t + 1], scale=1.0,
+                        )
+                    else:
+                        nc.scalar.activation(
+                            out=v_t[:, t, :], in_=acc[:], func=ACT.Tanh,
+                            bias=b_tau[:, t : t + 1], scale=0.5,
+                        )
+                if o == 0:
+                    nc.vector.tensor_tensor(
+                        out=a_t[:], in0=a_t[:], in1=h_T, op=ALU.subtract
+                    )
+            nc.vector.scalar_tensor_tensor(
+                out=v_t[:], in0=v_t[:], scalar=2.0, in1=a_t[:],
+                op0=ALU.subtract, op1=ALU.mult,
+            )
+            for t in range(4):
+                nc.vector.scalar_tensor_tensor(
+                    out=a_t[:, t, :], in0=v_t[:, t, :], scalar=neg_c[:, t : t + 1],
+                    in1=h_T[:, t, :], op0=ALU.mult, op1=ALU.add,
+                )
+            res[c] = a_t
+
+        def backward(c):
+            a_t = res[c]
+            o_sb = ep.tile([P, 4, 512], F32, name="o_sb", tag="o_sb")
+            for r in range(4):
+                bt = bt_psum.tile([P, 4, P], F32, name="bt", tag="bt")
+                for t in range(4):
+                    nc.tensor.transpose(
+                        bt[:, t, :], a_t[:, t, r * P : (r + 1) * P], ident[:]
+                    )
+                nc.scalar.copy(
+                    out=o_sb[:, r, :].rearrange("b (u p e) -> b u p e", u=2, e=2),
+                    in_=bt[:].rearrange("b (u e) p -> b u p e", u=2),
+                )
+            nc.sync.dma_start(
+                out=out[c * CHUNK : (c + 1) * CHUNK, :].rearrange("(p r) h -> p r h", r=4),
+                in_=o_sb[:],
+            )
+
+        for c in range(N_CHUNKS):
+            if c + 1 < N_CHUNKS:
+                forward(c + 1)
+            matmuls(c)
+            if c >= 1:
+                backward(c - 1)
+        backward(N_CHUNKS - 1)

@@ -33,6 +33,7 @@ def tile_liquidcell_pa_t_kernel(
         tp_psum = ctx.enter_context(tc.psum_pool(name="tp_psum", bufs=2))
         acc_psum = ctx.enter_context(tc.psum_pool(name="acc_psum", bufs=4))
         bt_psum = ctx.enter_context(tc.psum_pool(name="bt_psum", bufs=2))
+        ctx.enter_context(tc.manual_schedule())
 
         warm = const.tile([P, 1], F32, name="warm")
         nc.vector.memset(warm[:], 0.0)
@@ -105,46 +106,132 @@ def tile_liquidcell_pa_t_kernel(
                     bank[:].rearrange("p u b -> p b u"),
                 )
 
-        def quantise(grouped, codes, scales):
+        def quantise(unit):
+            grouped, codes, scales = unit
             nc.vector.quantize_mx(
                 out=codes[:].bitcast(FP8X4), scales=scales[:], in_=grouped[:]
             )
 
-        w_codes = {}
-        w_scales = {}
+        w_ops = {}
 
-        def prep_weight(o, g, src_words, engines):
+        def weight_unit(o, g, src_words, engines):
             gwt = grp.tile([P, 2048], BF16, name="gwt", tag="gw", align_bytes=64)
             transpose_group(src_words, gwt, engines)
-            w_codes[(o, g)] = wq.tile(
-                [P, 512], U32, name="w_codes%d%d" % (o, g), align_bytes=64
-            )
-            w_scales[(o, g)] = wq.tile(
-                [P, 512], U8, name="w_scales%d%d" % (o, g), align_bytes=64
-            )
-            quantise(gwt, w_codes[(o, g)], w_scales[(o, g)])
+            codes = wq.tile([P, 512], U32, name="w_codes%d%d" % (o, g), align_bytes=64)
+            scales = wq.tile([P, 512], U8, name="w_scales%d%d" % (o, g), align_bytes=64)
+            w_ops[(o, g)] = (codes, scales)
+            return (gwt, codes, scales)
 
-        act = {}
+        a_ops = {}
+        g_hid = {}
 
-        def forward(c):
+        def x_unit(c, engines):
             gx = grp.tile([P, 2048], BF16, name="gx", tag="gx", align_bytes=64)
-            gh = grp.tile([P, 2048], BF16, name="gh", tag="gh", bufs=3, align_bytes=64)
-            transpose_group(x_nat[c][:].bitcast(F32), gx, ("v", "s"))
-            transpose_group(h_nat[c][:].bitcast(F32), gh, ("s", "s"))
+            transpose_group(x_nat[c][:].bitcast(F32), gx, engines)
             xc = qp.tile([P, 512], U32, name="xc", tag="xc", align_bytes=64)
             xs = qp.tile([P, 512], U8, name="xs", tag="xs", align_bytes=64)
+            a_ops[(c, 0)] = (xc, xs)
+            return (gx, xc, xs)
+
+        def h_unit(c, engines):
+            gh = grp.tile([P, 2048], BF16, name="gh", tag="gh", bufs=3, align_bytes=64)
+            transpose_group(h_nat[c][:].bitcast(F32), gh, engines)
             hc = qp.tile([P, 512], U32, name="hc", tag="hc", align_bytes=64)
             hs = qp.tile([P, 512], U8, name="hs", tag="hs", align_bytes=64)
-            quantise(gx, xc, xs)
-            quantise(gh, hc, hs)
-            act[c] = (gh, ((xc, xs), (hc, hs)))
+            a_ops[(c, 1)] = (hc, hs)
+            g_hid[c] = gh
+            return (gh, hc, hs)
 
-        prep_weight(0, 0, win_nat[:].bitcast(F32), ("v", "s"))
-        prep_weight(0, 1, wrec_nat[:].bitcast(F32), ("v", "s"))
-        forward(0)
-        wtau_words = wtau_nat[:].bitcast(F32)
-        prep_weight(1, 0, wtau_words[:, :, 0:256], ("v", "s"))
-        prep_weight(1, 1, wtau_words[:, :, 256:512], ("v", "s"))
+        a_tiles = {}
+        v_tiles = {}
+
+        def h_T(c):
+            return g_hid[c][:].rearrange("p (b t) -> p t b", t=4)
+
+        def matmuls(c, o):
+            if o == 0:
+                dst = ep.tile([P, 4, 512], F32, name="a_t", tag="a_t", bufs=3)
+                a_tiles[c] = dst
+            else:
+                dst = ep.tile([P, 4, 512], F32, name="v_t", tag="v_t")
+                v_tiles[c] = dst
+            for t in range(4):
+                acc = acc_psum.tile([P, 512], F32, name="acc", tag="acc")
+                cols = slice(t * P, (t + 1) * P)
+                for g in range(2):
+                    nc.tensor.matmul_mx(
+                        out=acc[:],
+                        lhsT=w_ops[(o, g)][0][:, cols].bitcast(FP8X4),
+                        lhsT_scale=w_ops[(o, g)][1][:, cols],
+                        rhs=a_ops[(c, g)][0][:].bitcast(FP8X4),
+                        rhs_scale=a_ops[(c, g)][1][:],
+                        start=(g == 0),
+                        stop=(g == 1),
+                    )
+                if o == 0:
+                    nc.scalar.activation(
+                        out=dst[:, t, :], in_=acc[:], func=ACT.Tanh,
+                        bias=cst[:, t : t + 1], scale=1.0,
+                    )
+                else:
+                    nc.scalar.activation(
+                        out=dst[:, t, :], in_=acc[:], func=ACT.Tanh,
+                        bias=b_tau[:, t : t + 1], scale=0.5,
+                    )
+
+        def step1(c):
+            nc.vector.tensor_tensor(
+                out=a_tiles[c][:], in0=a_tiles[c][:], in1=h_T(c), op=ALU.subtract
+            )
+
+        def step2(c, cols):
+            nc.vector.scalar_tensor_tensor(
+                out=v_tiles[c][:, :, cols], in0=v_tiles[c][:, :, cols], scalar=2.0,
+                in1=a_tiles[c][:, :, cols], op0=ALU.subtract, op1=ALU.mult,
+            )
+
+        def step3(c, cols):
+            for t in range(4):
+                nc.vector.scalar_tensor_tensor(
+                    out=a_tiles[c][:, t, cols], in0=v_tiles[c][:, t, cols],
+                    scalar=neg_c[:, t : t + 1], in1=h_T(c)[:, t, cols],
+                    op0=ALU.mult, op1=ALU.add,
+                )
+
+        o_tiles = {}
+
+        def backward(c, rs, engines):
+            if c not in o_tiles:
+                o_tiles[c] = ep.tile([P, 4, 512], F32, name="o_sb", tag="o_sb")
+            o_sb = o_tiles[c]
+            for r, engine in zip(rs, engines):
+                bt = bt_psum.tile([P, 4, P], F32, name="bt", tag="bt")
+                for t in range(4):
+                    nc.tensor.transpose(
+                        bt[:, t, :], a_tiles[c][:, t, r * P : (r + 1) * P], ident[:]
+                    )
+                copy_on(
+                    engine,
+                    o_sb[:, r, :].rearrange("b (u p e) -> b u p e", u=2, e=2),
+                    bt[:].rearrange("b (u e) p -> b u p e", u=2),
+                )
+            nc.sync.dma_start(
+                out=out[c * CHUNK : (c + 1) * CHUNK, :].rearrange(
+                    "(p r) h -> p r h", r=4
+                )[:, rs[0] : rs[-1] + 1, :],
+                in_=o_sb[:, rs[0] : rs[-1] + 1, :],
+            )
+
+        ALL = slice(0, 512)
+        VS = ("v", "s")
+
+        u0 = weight_unit(0, 0, win_nat[:].bitcast(F32), VS)
+        u1 = weight_unit(0, 1, wrec_nat[:].bitcast(F32), VS)
+        quantise(u0)
+        u2 = x_unit(0, VS)
+        quantise(u1)
+        u3 = h_unit(0, VS)
+        quantise(u2)
 
         vt = tp_psum.tile([P, 2, 256], F32, name="vt", tag="tp")
         nc.tensor.transpose(vt[:, 0, 0:P], vec_rows[:].bitcast(F32), ident[:])
@@ -161,75 +248,42 @@ def tile_liquidcell_pa_t_kernel(
         nc.vector.reciprocal(out=inv_tb[:], in_=cst[:, 4:8])
         neg_c = const.tile([P, 4], F32, name="neg_c")
         nc.vector.tensor_scalar_mul(out=neg_c[:], in0=inv_tb[:], scalar1=-1.0 / 15.0)
+        quantise(u3)
 
-        res = {}
+        matmuls(0, 0)
+        wtau_words = wtau_nat[:].bitcast(F32)
+        u4 = weight_unit(1, 0, wtau_words[:, :, 0:256], VS)
+        u5 = weight_unit(1, 1, wtau_words[:, :, 256:512], VS)
+        quantise(u4)
+        u6 = x_unit(1, VS)
+        quantise(u5)
+        u7 = h_unit(1, VS)
+        step1(0)
+        quantise(u6)
+        quantise(u7)
+        matmuls(0, 1)
+        step2(0, ALL)
 
-        def matmuls(c):
-            gh, ops = act[c]
-            a_t = ep.tile([P, 4, 512], F32, name="a_t", tag="a_t", bufs=3)
-            v_t = ep.tile([P, 4, 512], F32, name="v_t", tag="v_t")
-            h_T = gh[:].rearrange("p (b t) -> p t b", t=4)
-            for o in range(2):
-                for t in range(4):
-                    acc = acc_psum.tile([P, 512], F32, name="acc", tag="acc")
-                    cols = slice(t * P, (t + 1) * P)
-                    for g in range(2):
-                        nc.tensor.matmul_mx(
-                            out=acc[:],
-                            lhsT=w_codes[(o, g)][:, cols].bitcast(FP8X4),
-                            lhsT_scale=w_scales[(o, g)][:, cols],
-                            rhs=ops[g][0][:].bitcast(FP8X4),
-                            rhs_scale=ops[g][1][:],
-                            start=(g == 0),
-                            stop=(g == 1),
-                        )
-                    if o == 0:
-                        nc.scalar.activation(
-                            out=a_t[:, t, :], in_=acc[:], func=ACT.Tanh,
-                            bias=cst[:, t : t + 1], scale=1.0,
-                        )
-                    else:
-                        nc.scalar.activation(
-                            out=v_t[:, t, :], in_=acc[:], func=ACT.Tanh,
-                            bias=b_tau[:, t : t + 1], scale=0.5,
-                        )
-                if o == 0:
-                    nc.vector.tensor_tensor(
-                        out=a_t[:], in0=a_t[:], in1=h_T, op=ALU.subtract
-                    )
-            nc.vector.scalar_tensor_tensor(
-                out=v_t[:], in0=v_t[:], scalar=2.0, in1=a_t[:],
-                op0=ALU.subtract, op1=ALU.mult,
-            )
-            for t in range(4):
-                nc.vector.scalar_tensor_tensor(
-                    out=a_t[:, t, :], in0=v_t[:, t, :], scalar=neg_c[:, t : t + 1],
-                    in1=h_T[:, t, :], op0=ALU.mult, op1=ALU.add,
-                )
-            res[c] = a_t
-
-        def backward(c):
-            a_t = res[c]
-            o_sb = ep.tile([P, 4, 512], F32, name="o_sb", tag="o_sb")
-            for r in range(4):
-                bt = bt_psum.tile([P, 4, P], F32, name="bt", tag="bt")
-                for t in range(4):
-                    nc.tensor.transpose(
-                        bt[:, t, :], a_t[:, t, r * P : (r + 1) * P], ident[:]
-                    )
-                nc.scalar.copy(
-                    out=o_sb[:, r, :].rearrange("b (u p e) -> b u p e", u=2, e=2),
-                    in_=bt[:].rearrange("b (u e) p -> b u p e", u=2),
-                )
-            nc.sync.dma_start(
-                out=out[c * CHUNK : (c + 1) * CHUNK, :].rearrange("(p r) h -> p r h", r=4),
-                in_=o_sb[:],
-            )
-
-        for c in range(N_CHUNKS):
+        for c in range(1, N_CHUNKS):
             if c + 1 < N_CHUNKS:
-                forward(c + 1)
-            matmuls(c)
-            if c >= 1:
-                backward(c - 1)
-        backward(N_CHUNKS - 1)
+                ux = x_unit(c + 1, VS)
+                uh = h_unit(c + 1, ("s", "s"))
+            step3(c - 1, ALL)
+            if c + 1 < N_CHUNKS:
+                quantise(ux)
+                quantise(uh)
+            matmuls(c, 0)
+            step1(c)
+            matmuls(c, 1)
+            if c + 1 < N_CHUNKS:
+                step2(c, ALL)
+                backward(c - 1, (0, 1, 2, 3), ("s", "s", "s", "s"))
+            else:
+                step2(c, slice(0, 256))
+                backward(c - 1, (0, 1, 2, 3), ("s", "s", "s", "s"))
+        last = N_CHUNKS - 1
+        step3(last, slice(0, 256))
+        step2(last, slice(256, 512))
+        backward(last, (0, 1), ("s", "s"))
+        step3(last, slice(256, 512))
+        backward(last, (2, 3), ("s", "v"))

@@ -30,9 +30,8 @@ def tile_liquidcell_pa_t_kernel(
         grp = ctx.enter_context(tc.tile_pool(name="grp", bufs=2))
         qp = ctx.enter_context(tc.tile_pool(name="qp", bufs=2))
         ep = ctx.enter_context(tc.tile_pool(name="ep", bufs=2))
-        tp_psum = ctx.enter_context(tc.psum_pool(name="tp_psum", bufs=2))
+        tp_psum = ctx.enter_context(tc.psum_pool(name="tp_psum", bufs=4))
         acc_psum = ctx.enter_context(tc.psum_pool(name="acc_psum", bufs=4))
-        bt_psum = ctx.enter_context(tc.psum_pool(name="bt_psum", bufs=2))
         ctx.enter_context(tc.manual_schedule())
 
         warm = const.tile([P, 1], F32, name="warm")
@@ -205,7 +204,7 @@ def tile_liquidcell_pa_t_kernel(
                 o_tiles[c] = ep.tile([P, 4, 512], F32, name="o_sb", tag="o_sb")
             o_sb = o_tiles[c]
             for r, engine in zip(rs, engines):
-                bt = bt_psum.tile([P, 4, P], F32, name="bt", tag="bt")
+                bt = tp_psum.tile([P, 4, P], F32, name="bt", tag="tp")
                 for t in range(4):
                     nc.tensor.transpose(
                         bt[:, t, :], a_tiles[c][:, t, r * P : (r + 1) * P], ident[:]
@@ -215,11 +214,13 @@ def tile_liquidcell_pa_t_kernel(
                     o_sb[:, r, :].rearrange("b (u p e) -> b u p e", u=2, e=2),
                     bt[:].rearrange("b (u e) p -> b u p e", u=2),
                 )
+
+        def store(c, r0, r1):
             nc.sync.dma_start(
                 out=out[c * CHUNK : (c + 1) * CHUNK, :].rearrange(
                     "(p r) h -> p r h", r=4
-                )[:, rs[0] : rs[-1] + 1, :],
-                in_=o_sb[:, rs[0] : rs[-1] + 1, :],
+                )[:, r0:r1, :],
+                in_=o_tiles[c][:, r0:r1, :],
             )
 
         ALL = slice(0, 512)
@@ -262,28 +263,38 @@ def tile_liquidcell_pa_t_kernel(
         quantise(u6)
         quantise(u7)
         matmuls(0, 1)
-        step2(0, ALL)
 
+        SS = ("s", "s")
+        LAG = 2
         for c in range(1, N_CHUNKS):
-            if c + 1 < N_CHUNKS:
+            more = c + 1 < N_CHUNKS
+            if more:
                 ux = x_unit(c + 1, VS)
-                uh = h_unit(c + 1, ("s", "s"))
+            if c - LAG >= 0:
+                backward(c - LAG, (0, 1), SS)
+            step2(c - 1, ALL)
             step3(c - 1, ALL)
-            if c + 1 < N_CHUNKS:
-                quantise(ux)
-                quantise(uh)
             matmuls(c, 0)
+            if more:
+                uh = h_unit(c + 1, SS)
+            if c - LAG >= 0:
+                backward(c - LAG, (2, 3), SS)
+                store(c - LAG, 0, 4)
+            if more:
+                quantise(ux)
             step1(c)
+            if more:
+                quantise(uh)
             matmuls(c, 1)
-            if c + 1 < N_CHUNKS:
-                step2(c, ALL)
-                backward(c - 1, (0, 1, 2, 3), ("s", "s", "s", "s"))
-            else:
-                step2(c, slice(0, 256))
-                backward(c - 1, (0, 1, 2, 3), ("s", "s", "s", "s"))
+
         last = N_CHUNKS - 1
+        backward(last - 1, (0, 1, 2, 3), ("s", "s", "s", "s"))
+        store(last - 1, 0, 4)
+        step2(last, slice(0, 256))
         step3(last, slice(0, 256))
         step2(last, slice(256, 512))
-        backward(last, (0, 1), ("s", "s"))
+        backward(last, (0, 1), SS)
+        store(last, 0, 2)
         step3(last, slice(256, 512))
         backward(last, (2, 3), ("s", "v"))
+        store(last, 2, 4)

@@ -225,6 +225,7 @@ def tile_liquidcell_pa_t_kernel(
 
         ALL = slice(0, 512)
         VS = ("v", "s")
+        SS = ("s", "s")
 
         u0 = weight_unit(0, 0, win_nat[:].bitcast(F32), VS)
         u1 = weight_unit(0, 1, wrec_nat[:].bitcast(F32), VS)
@@ -256,20 +257,19 @@ def tile_liquidcell_pa_t_kernel(
         u4 = weight_unit(1, 0, wtau_words[:, :, 0:256], VS)
         u5 = weight_unit(1, 1, wtau_words[:, :, 256:512], VS)
         quantise(u4)
-        u6 = x_unit(1, VS)
+        u6 = x_unit(1, SS)
         quantise(u5)
-        u7 = h_unit(1, VS)
+        u7 = h_unit(1, SS)
         step1(0)
         quantise(u6)
         quantise(u7)
         matmuls(0, 1)
 
-        SS = ("s", "s")
         LAG = 2
         for c in range(1, N_CHUNKS):
             more = c + 1 < N_CHUNKS
             if more:
-                ux = x_unit(c + 1, VS)
+                ux = x_unit(c + 1, SS if c % 2 == 1 else VS)
             if c - LAG >= 0:
                 backward(c - LAG, (0, 1), SS)
             step2(c - 1, ALL)
@@ -295,6 +295,9 @@ def tile_liquidcell_pa_t_kernel(
         step2(last, slice(256, 512))
         backward(last, (0, 1), SS)
         store(last, 0, 2)
-        step3(last, slice(256, 512))
-        backward(last, (2, 3), ("s", "v"))
-        store(last, 2, 4)
+        step3(last, slice(256, 384))
+        backward(last, (2,), ("s",))
+        store(last, 2, 3)
+        step3(last, slice(384, 512))
+        backward(last, (3,), ("s",))
+        store(last, 3, 4)

@@ -273,6 +273,8 @@ def tile_liquidcell_pa_t_kernel(
             if c - LAG >= 0:
                 backward(c - LAG, (0, 1), SS)
             step2(c - 1, ALL)
+            if more:
+                quantise(ux)
             step3(c - 1, ALL)
             matmuls(c, 0)
             if more:
@@ -280,8 +282,6 @@ def tile_liquidcell_pa_t_kernel(
             if c - LAG >= 0:
                 backward(c - LAG, (2, 3), SS)
                 store(c - LAG, 0, 4)
-            if more:
-                quantise(ux)
             step1(c)
             if more:
                 quantise(uh)
@@ -291,8 +291,8 @@ def tile_liquidcell_pa_t_kernel(
         backward(last - 1, (0, 1, 2, 3), ("s", "s", "s", "s"))
         store(last - 1, 0, 4)
         step2(last, slice(0, 256))
-        step3(last, slice(0, 256))
         step2(last, slice(256, 512))
+        step3(last, slice(0, 256))
         backward(last, (0, 1), SS)
         store(last, 0, 2)
         step3(last, slice(256, 384))

@@ -44,15 +44,18 @@ def tile_liquidcell_pa_t_kernel(
 
         vec_rows = const.tile([P, 256], BF16, name="vec_rows")
         nc.vector.memset(vec_rows[:], 0.0)
-        for i, vec in enumerate((W_in_b, tau_base, tau_adapt_b)):
-            nc.scalar.dma_start(
-                out=vec_rows[2 * i : 2 * i + 2, :],
-                in_=vec.rearrange("(u w) -> u w", u=2),
-            )
+
+        def load_vectors():
+            for i, vec in enumerate((W_in_b, tau_base, tau_adapt_b)):
+                nc.sync.dma_start(
+                    out=vec_rows[2 * i : 2 * i + 2, :],
+                    in_=vec.rearrange("(u w) -> u w", u=2),
+                )
 
         win_nat = nat.tile([P, 4, 512], BF16, name="win_nat")
         wrec_nat = nat.tile([P, 4, 512], BF16, name="wrec_nat")
-        wtau_nat = nat.tile([P, 4, 1024], BF16, name="wtau_nat")
+        wtx_nat = nat.tile([P, 4, 512], BF16, name="wtx_nat")
+        wth_nat = nat.tile([P, 4, 512], BF16, name="wth_nat")
         x_nat = []
         h_nat = []
         for c in range(N_CHUNKS):
@@ -65,21 +68,38 @@ def tile_liquidcell_pa_t_kernel(
                 in_=src.rearrange("(u p e) k -> p u e k", u=2, e=2),
             )
 
-        def load_chunk(c):
+        def load_tau_rows(dst, u, cols):
+            nc.sync.dma_start(
+                out=dst[:, 2 * u : 2 * u + 2, :],
+                in_=tau_adapt_w[u * 256 : (u + 1) * 256, cols].rearrange(
+                    "(p e) k -> p e k", e=2
+                ),
+            )
+
+        def load_x(c):
             rows = slice(c * CHUNK, (c + 1) * CHUNK)
             nc.sync.dma_start(
                 out=x_nat[c][:], in_=x[rows, :].rearrange("(p r) k -> p r k", r=4)
             )
+
+        def load_h(c):
+            rows = slice(c * CHUNK, (c + 1) * CHUNK)
             nc.sync.dma_start(
                 out=h_nat[c][:], in_=hidden[rows, :].rearrange("(p r) k -> p r k", r=4)
             )
 
         load_weight(win_nat, W_in_w)
+        load_x(0)
+        load_vectors()
         load_weight(wrec_nat, W_rec)
-        load_chunk(0)
-        load_weight(wtau_nat, tau_adapt_w)
+        load_h(0)
+        for u in range(2):
+            load_tau_rows(wtx_nat, u, slice(0, I))
+        for u in range(2):
+            load_tau_rows(wth_nat, u, slice(I, I + H))
         for c in range(1, N_CHUNKS):
-            load_chunk(c)
+            load_x(c)
+            load_h(c)
 
         def copy_on(engine, dst, src):
             if engine == "v":
@@ -143,77 +163,103 @@ def tile_liquidcell_pa_t_kernel(
 
         a_tiles = {}
         v_tiles = {}
-
-        def h_T(c):
-            return g_hid[c][:].rearrange("p (b t) -> p t b", t=4)
-
-        def matmuls(c, o):
-            if o == 0:
-                dst = ep.tile([P, 4, 512], F32, name="a_t", tag="a_t", bufs=3)
-                a_tiles[c] = dst
-            else:
-                dst = ep.tile([P, 4, 512], F32, name="v_t", tag="v_t")
-                v_tiles[c] = dst
-            for t in range(4):
-                acc = acc_psum.tile([P, 512], F32, name="acc", tag="acc")
-                cols = slice(t * P, (t + 1) * P)
-                for g in range(2):
-                    nc.tensor.matmul_mx(
-                        out=acc[:],
-                        lhsT=w_ops[(o, g)][0][:, cols].bitcast(FP8X4),
-                        lhsT_scale=w_ops[(o, g)][1][:, cols],
-                        rhs=a_ops[(c, g)][0][:].bitcast(FP8X4),
-                        rhs_scale=a_ops[(c, g)][1][:],
-                        start=(g == 0),
-                        stop=(g == 1),
-                    )
-                if o == 0:
-                    nc.scalar.activation(
-                        out=dst[:, t, :], in_=acc[:], func=ACT.Tanh,
-                        bias=cst[:, t : t + 1], scale=1.0,
-                    )
-                else:
-                    nc.scalar.activation(
-                        out=dst[:, t, :], in_=acc[:], func=ACT.Tanh,
-                        bias=b_tau[:, t : t + 1], scale=0.5,
-                    )
-
-        def step1(c):
-            nc.vector.tensor_tensor(
-                out=a_tiles[c][:], in0=a_tiles[c][:], in1=h_T(c), op=ALU.subtract
-            )
-
-        def step2(c, cols):
-            nc.vector.scalar_tensor_tensor(
-                out=v_tiles[c][:, :, cols], in0=v_tiles[c][:, :, cols], scalar=2.0,
-                in1=a_tiles[c][:, :, cols], op0=ALU.subtract, op1=ALU.mult,
-            )
-
-        def step3(c, cols):
-            for t in range(4):
-                nc.vector.scalar_tensor_tensor(
-                    out=a_tiles[c][:, t, cols], in0=v_tiles[c][:, t, cols],
-                    scalar=neg_c[:, t : t + 1], in1=h_T(c)[:, t, cols],
-                    op0=ALU.mult, op1=ALU.add,
-                )
-
         o_tiles = {}
 
-        def backward(c, rs, engines):
-            if c not in o_tiles:
-                o_tiles[c] = ep.tile([P, 4, 512], F32, name="o_sb", tag="o_sb")
-            o_sb = o_tiles[c]
-            for r, engine in zip(rs, engines):
-                bt = tp_psum.tile([P, 4, P], F32, name="bt", tag="tp")
-                for t in range(4):
-                    nc.tensor.transpose(
-                        bt[:, t, :], a_tiles[c][:, t, r * P : (r + 1) * P], ident[:]
-                    )
-                copy_on(
-                    engine,
-                    o_sb[:, r, :].rearrange("b (u p e) -> b u p e", u=2, e=2),
-                    bt[:].rearrange("b (u e) p -> b u p e", u=2),
+        def mm_pass(acc, c, o, g, t):
+            cols = slice(t * P, (t + 1) * P)
+            nc.tensor.matmul_mx(
+                out=acc[:],
+                lhsT=w_ops[(o, g)][0][:, cols].bitcast(FP8X4),
+                lhsT_scale=w_ops[(o, g)][1][:, cols],
+                rhs=a_ops[(c, g)][0][:].bitcast(FP8X4),
+                rhs_scale=a_ops[(c, g)][1][:],
+                start=(g == 0),
+                stop=(g == 1),
+            )
+
+        def new_acc():
+            acc = acc_psum.tile([P, 512], F32, name="acc", tag="acc")
+            return acc
+
+        def tanh_out(acc, c, o, t):
+            if o == 0:
+                nc.scalar.activation(
+                    out=a_tiles[c][:, t, :], in_=acc[:], func=ACT.Tanh,
+                    bias=cst[:, t : t + 1], scale=1.0,
                 )
+            else:
+                nc.scalar.activation(
+                    out=v_tiles[c][:, t, :], in_=acc[:], func=ACT.Tanh,
+                    bias=b_tau[:, t : t + 1], scale=0.5,
+                )
+
+        def new_elementwise(c, o):
+            if o == 0:
+                a_t = ep.tile([P, 4, 512], F32, name="a_t", tag="a_t", bufs=3)
+                a_tiles[c] = a_t
+            else:
+                v_t = ep.tile([P, 4, 512], F32, name="v_t", tag="v_t", bufs=3)
+                v_tiles[c] = v_t
+
+        def matmuls(c, o):
+            new_elementwise(c, o)
+            for t in range(4):
+                acc = new_acc()
+                for g in range(2):
+                    mm_pass(acc, c, o, g, t)
+                tanh_out(acc, c, o, t)
+
+        def diff(c):
+            nc.vector.tensor_tensor(
+                out=a_tiles[c][:], in0=a_tiles[c][:],
+                in1=g_hid[c][:].rearrange("p (b t) -> p t b", t=4), op=ALU.subtract,
+            )
+
+        def weight_v(c, t, engine):
+            if engine == "v":
+                nc.vector.tensor_scalar(
+                    out=v_tiles[c][:, t, :], in0=v_tiles[c][:, t, :],
+                    scalar1=neg_c[:, t : t + 1], scalar2=two_c[:, t : t + 1],
+                    op0=ALU.mult, op1=ALU.add,
+                )
+            elif engine == "g":
+                nc.gpsimd.tensor_scalar(
+                    out=v_tiles[c][:, t, :], in0=v_tiles[c][:, t, :],
+                    scalar1=neg_c[:, t : t + 1], scalar2=two_c[:, t : t + 1],
+                    op0=ALU.mult, op1=ALU.add,
+                )
+            else:
+                nc.scalar.activation(
+                    out=v_tiles[c][:, t, :], in_=v_tiles[c][:, t, :], func=ACT.Identity,
+                    bias=two_c[:, t : t + 1], scale=neg_c[:, t : t + 1],
+                )
+
+        def prod(c, cols):
+            nc.vector.tensor_tensor(
+                out=v_tiles[c][:, :, cols], in0=v_tiles[c][:, :, cols],
+                in1=a_tiles[c][:, :, cols], op=ALU.mult,
+            )
+
+        b_banks = {}
+
+        def back(c, r):
+            bt = tp_psum.tile([P, 4, P], F32, name="bt", tag="tp")
+            for t in range(4):
+                nc.tensor.transpose(
+                    bt[:, t, :], v_tiles[c][:, t, r * P : (r + 1) * P], ident[:]
+                )
+            b_banks[(c, r)] = bt
+
+        def finish(c, r):
+            if c not in o_tiles:
+                o_sb = ep.tile([P, 4, 512], F32, name="o_sb", tag="o_sb")
+                o_tiles[c] = o_sb
+            nc.vector.tensor_tensor(
+                out=o_tiles[c][:, r, :].rearrange("b (u p e) -> b u p e", u=2, e=2),
+                in0=b_banks[(c, r)][:].rearrange("b (u e) p -> b u p e", u=2),
+                in1=h_nat[c][:, r, :].rearrange("b (u p e) -> b u p e", u=2, e=2),
+                op=ALU.add,
+            )
 
         def store(c, r0, r1):
             nc.sync.dma_start(
@@ -228,12 +274,14 @@ def tile_liquidcell_pa_t_kernel(
         SS = ("s", "s")
 
         u0 = weight_unit(0, 0, win_nat[:].bitcast(F32), VS)
-        u1 = weight_unit(0, 1, wrec_nat[:].bitcast(F32), VS)
+        u1 = x_unit(0, VS)
         quantise(u0)
-        u2 = x_unit(0, VS)
+        u2 = weight_unit(0, 1, wrec_nat[:].bitcast(F32), VS)
         quantise(u1)
         u3 = h_unit(0, VS)
         quantise(u2)
+        u4 = weight_unit(1, 0, wtx_nat[:].bitcast(F32), VS)
+        quantise(u3)
 
         vt = tp_psum.tile([P, 2, 256], F32, name="vt", tag="tp")
         nc.tensor.transpose(vt[:, 0, 0:P], vec_rows[:].bitcast(F32), ident[:])
@@ -250,54 +298,62 @@ def tile_liquidcell_pa_t_kernel(
         nc.vector.reciprocal(out=inv_tb[:], in_=cst[:, 4:8])
         neg_c = const.tile([P, 4], F32, name="neg_c")
         nc.vector.tensor_scalar_mul(out=neg_c[:], in0=inv_tb[:], scalar1=-1.0 / 15.0)
-        quantise(u3)
+        two_c = const.tile([P, 4], F32, name="two_c")
+        nc.vector.tensor_scalar_mul(out=two_c[:], in0=inv_tb[:], scalar1=2.0 / 15.0)
 
-        matmuls(0, 0)
-        wtau_words = wtau_nat[:].bitcast(F32)
-        u4 = weight_unit(1, 0, wtau_words[:, :, 0:256], VS)
-        u5 = weight_unit(1, 1, wtau_words[:, :, 256:512], VS)
+        new_elementwise(0, 0)
+        acc0 = [new_acc(), new_acc(), new_acc(), new_acc()]
+        for t in range(4):
+            mm_pass(acc0[t], 0, 0, 0, t)
+        u5 = weight_unit(1, 1, wth_nat[:].bitcast(F32), VS)
+        for t in range(4):
+            mm_pass(acc0[t], 0, 0, 1, t)
+            tanh_out(acc0[t], 0, 0, t)
         quantise(u4)
         u6 = x_unit(1, SS)
         quantise(u5)
         u7 = h_unit(1, SS)
-        step1(0)
-        quantise(u6)
-        quantise(u7)
         matmuls(0, 1)
+        quantise(u6)
+        diff(0)
+        quantise(u7)
 
-        LAG = 2
+        W_ENGINES = ("s", "s", "g", "g")
+        def weights(c, which):
+            for t in range(4):
+                if W_ENGINES[t] == which:
+                    weight_v(c, t, which)
+
+        weights(0, "s")
+        weights(0, "g")
         for c in range(1, N_CHUNKS):
             more = c + 1 < N_CHUNKS
-            if more:
-                ux = x_unit(c + 1, SS if c % 2 == 1 else VS)
-            if c - LAG >= 0:
-                backward(c - LAG, (0, 1), SS)
-            step2(c - 1, ALL)
-            if more:
-                quantise(ux)
-            step3(c - 1, ALL)
+            if c >= 2:
+                for r in range(4):
+                    finish(c - 2, r)
+                store(c - 2, 0, 4)
             matmuls(c, 0)
             if more:
+                ux = x_unit(c + 1, SS)
                 uh = h_unit(c + 1, SS)
-            if c - LAG >= 0:
-                backward(c - LAG, (2, 3), SS)
-                store(c - LAG, 0, 4)
-            step1(c)
-            if more:
-                quantise(uh)
+            prod(c - 1, ALL)
             matmuls(c, 1)
+            weights(c, "s")
+            weights(c, "g")
+            if more:
+                quantise(ux)
+                quantise(uh)
+            diff(c)
+            for r in range(4):
+                back(c - 1, r)
 
         last = N_CHUNKS - 1
-        backward(last - 1, (0, 1, 2, 3), ("s", "s", "s", "s"))
+        for r in range(4):
+            finish(last - 1, r)
         store(last - 1, 0, 4)
-        step2(last, slice(0, 256))
-        step2(last, slice(256, 512))
-        step3(last, slice(0, 256))
-        backward(last, (0, 1), SS)
-        store(last, 0, 2)
-        step3(last, slice(256, 384))
-        backward(last, (2,), ("s",))
-        store(last, 2, 3)
-        step3(last, slice(384, 512))
-        backward(last, (3,), ("s",))
-        store(last, 3, 4)
+        for r in range(4):
+            prod(last, slice(r * P, (r + 1) * P))
+            back(last, r)
+        for r in range(4):
+            finish(last, r)
+            store(last, r, r + 1)

@@ -41,6 +41,8 @@ def tile_liquidcell_pa_t_kernel(
 
         ident = const.tile([P, P], F32, name="ident")
         masks.make_identity(nc, ident[:])
+        ident_h = const.tile([P, P], BF16, name="ident_h")
+        masks.make_identity(nc, ident_h[:])
 
         vec_rows = const.tile([P, 256], BF16, name="vec_rows")
         nc.vector.memset(vec_rows[:], 0.0)
@@ -209,29 +211,27 @@ def tile_liquidcell_pa_t_kernel(
                     mm_pass(acc, c, o, g, t)
                 tanh_out(acc, c, o, t)
 
-        def diff(c):
-            nc.vector.tensor_tensor(
-                out=a_tiles[c][:], in0=a_tiles[c][:],
-                in1=g_hid[c][:].rearrange("p (b t) -> p t b", t=4), op=ALU.subtract,
+        def h_T(c):
+            return g_hid[c][:].rearrange("p (b t) -> p t b", t=4)
+
+        def diff(c, ts, engine):
+            engine.tensor_tensor(
+                out=a_tiles[c][:, ts, :], in0=a_tiles[c][:, ts, :],
+                in1=h_T(c)[:, ts, :], op=ALU.subtract,
             )
 
         def weight_v(c, t, engine):
-            if engine == "v":
-                nc.vector.tensor_scalar(
-                    out=v_tiles[c][:, t, :], in0=v_tiles[c][:, t, :],
-                    scalar1=neg_c[:, t : t + 1], scalar2=two_c[:, t : t + 1],
-                    op0=ALU.mult, op1=ALU.add,
-                )
-            elif engine == "g":
-                nc.gpsimd.tensor_scalar(
-                    out=v_tiles[c][:, t, :], in0=v_tiles[c][:, t, :],
-                    scalar1=neg_c[:, t : t + 1], scalar2=two_c[:, t : t + 1],
-                    op0=ALU.mult, op1=ALU.add,
-                )
-            else:
+            if engine == "s":
                 nc.scalar.activation(
                     out=v_tiles[c][:, t, :], in_=v_tiles[c][:, t, :], func=ACT.Identity,
                     bias=two_c[:, t : t + 1], scale=neg_c[:, t : t + 1],
+                )
+            else:
+                eng = nc.vector if engine == "v" else nc.gpsimd
+                eng.tensor_scalar(
+                    out=v_tiles[c][:, t, :], in0=v_tiles[c][:, t, :],
+                    scalar1=neg_c[:, t : t + 1], scalar2=two_c[:, t : t + 1],
+                    op0=ALU.mult, op1=ALU.add,
                 )
 
         def prod(c, cols):
@@ -240,7 +240,29 @@ def tile_liquidcell_pa_t_kernel(
                 in1=a_tiles[c][:, :, cols], op=ALU.mult,
             )
 
+        def prod_last(c, cols):
+            nc.vector.scalar_tensor_tensor(
+                out=v_tiles[c][:, :, cols], in0=v_tiles[c][:, :, cols], scalar=2.0,
+                in1=a_tiles[c][:, :, cols], op0=ALU.subtract, op1=ALU.mult,
+            )
+
         b_banks = {}
+
+        def back_h(c, r):
+            bt = tp_psum.tile([P, 4, P], F32, name="bt", tag="tp")
+            nc.tensor.matmul(
+                bt[:].rearrange("b t p -> b (t p)"), lhsT=ident_h[:],
+                rhs=h_nat[c][:, r, :].rearrange("b (u p e) -> b u e p", u=2, e=2),
+                start=True, stop=False,
+            )
+            b_banks[(c, r)] = bt
+
+        def back_p(c, r):
+            for t in range(4):
+                nc.tensor.matmul(
+                    b_banks[(c, r)][:, t, :], lhsT=v_tiles[c][:, t, r * P : (r + 1) * P],
+                    rhs=ident[:], start=False, stop=(t == 3), is_transpose=True,
+                )
 
         def back(c, r):
             bt = tp_psum.tile([P, 4, P], F32, name="bt", tag="tp")
@@ -250,15 +272,25 @@ def tile_liquidcell_pa_t_kernel(
                 )
             b_banks[(c, r)] = bt
 
-        def finish(c, r):
+        def o_tile(c):
             if c not in o_tiles:
                 o_sb = ep.tile([P, 4, 512], F32, name="o_sb", tag="o_sb")
                 o_tiles[c] = o_sb
+            return o_tiles[c]
+
+        def finish(c, r):
             nc.vector.tensor_tensor(
-                out=o_tiles[c][:, r, :].rearrange("b (u p e) -> b u p e", u=2, e=2),
+                out=o_tile(c)[:, r, :].rearrange("b (u p e) -> b u p e", u=2, e=2),
                 in0=b_banks[(c, r)][:].rearrange("b (u e) p -> b u p e", u=2),
                 in1=h_nat[c][:, r, :].rearrange("b (u p e) -> b u p e", u=2, e=2),
                 op=ALU.add,
+            )
+
+        def finish_s(c, r, engine):
+            copy_on(
+                engine,
+                o_tile(c)[:, r, :].rearrange("b (u p e) -> b u p e", u=2, e=2),
+                b_banks[(c, r)][:].rearrange("b (u e) p -> b u p e", u=2),
             )
 
         def store(c, r0, r1):
@@ -310,50 +342,66 @@ def tile_liquidcell_pa_t_kernel(
             mm_pass(acc0[t], 0, 0, 1, t)
             tanh_out(acc0[t], 0, 0, t)
         quantise(u4)
-        u6 = x_unit(1, SS)
         quantise(u5)
-        u7 = h_unit(1, SS)
-        matmuls(0, 1)
+        u6 = x_unit(1, ("v", "v"))
+        u7 = h_unit(1, ("v", "s"))
         quantise(u6)
-        diff(0)
         quantise(u7)
+        matmuls(0, 1)
+        diff(0, slice(0, 4), nc.vector)
 
-        W_ENGINES = ("s", "s", "g", "g")
-        def weights(c, which):
+        def weights(c, engines):
             for t in range(4):
-                if W_ENGINES[t] == which:
-                    weight_v(c, t, which)
+                weight_v(c, t, engines[t])
 
-        weights(0, "s")
-        weights(0, "g")
+        weights(0, ("s", "s", "v", "v"))
+        last = N_CHUNKS - 1
+        K = 0
+        D3 = False
         for c in range(1, N_CHUNKS):
             more = c + 1 < N_CHUNKS
             if c >= 2:
                 for r in range(4):
-                    finish(c - 2, r)
-                store(c - 2, 0, 4)
+                    if r < 4 - K:
+                        finish(c - 2, r)
             matmuls(c, 0)
+            if c >= 2:
+                for r in range(4 - K, 4):
+                    finish_s(c - 2, r, "s")
+                store(c - 2, 0, 4)
             if more:
                 ux = x_unit(c + 1, SS)
                 uh = h_unit(c + 1, SS)
             prod(c - 1, ALL)
             matmuls(c, 1)
-            weights(c, "s")
-            weights(c, "g")
             if more:
+                weights(c, ("s", "s", "g", "g"))
                 quantise(ux)
                 quantise(uh)
-            diff(c)
+            if D3 and more:
+                diff(c, slice(0, 3), nc.vector)
+                diff(c, slice(3, 4), nc.gpsimd)
+            else:
+                diff(c, slice(0, 4), nc.vector)
+            if not more:
+                weights(c, ("s", "s", "s", "s"))
             for r in range(4):
-                back(c - 1, r)
+                if r < 4 - K - (c == last) * 2:
+                    back(c - 1, r)
+                else:
+                    back_h(c - 1, r)
+                    back_p(c - 1, r)
 
-        last = N_CHUNKS - 1
         for r in range(4):
-            finish(last - 1, r)
+            if r < 4 - K - 2:
+                finish(last - 1, r)
+            else:
+                finish_s(last - 1, r, "s")
         store(last - 1, 0, 4)
         for r in range(4):
-            prod(last, slice(r * P, (r + 1) * P))
-            back(last, r)
+            back_h(last, r)
         for r in range(4):
-            finish(last, r)
+            prod(last, slice(r * P, (r + 1) * P))
+            back_p(last, r)
+            finish_s(last, r, "s")
             store(last, r, r + 1)

@@ -14,8 +14,8 @@ ACT = mybir.ActivationFunctionType
 
 P = 128
 B, I, H = 4096, 512, 512
-CHUNK = 512
-N_CHUNKS = B // CHUNK
+CHUNKS = (512, 512, 512, 512, 512, 512, 512, 512)
+N_CHUNKS = len(CHUNKS)
 FLOPS = 4 * 2 * B * 512 * 512
 
 
@@ -60,9 +60,16 @@ def tile_liquidcell_pa_t_kernel(
         wth_nat = nat.tile([P, 4, 512], BF16, name="wth_nat")
         x_nat = []
         h_nat = []
-        for c in range(N_CHUNKS):
-            x_nat.append(nat.tile([P, 4, 512], BF16, name="x_nat%d" % c))
-            h_nat.append(nat.tile([P, 4, 512], BF16, name="h_nat%d" % c))
+        row0 = []
+        for c, n in enumerate(CHUNKS):
+            row0.append(sum(CHUNKS[0:c]))
+            x_nat.append(nat.tile([P, n // P, 512], BF16, name="x_nat%d" % c))
+            h_nat.append(nat.tile([P, n // P, 512], BF16, name="h_nat%d" % c))
+
+        def chunk_rows(src, c):
+            return src[row0[c] : row0[c] + CHUNKS[c], :].rearrange(
+                "(p r) k -> p r k", r=CHUNKS[c] // P
+            )
 
         def load_weight(dst, src):
             nc.sync.dma_start(
@@ -79,16 +86,10 @@ def tile_liquidcell_pa_t_kernel(
             )
 
         def load_x(c):
-            rows = slice(c * CHUNK, (c + 1) * CHUNK)
-            nc.sync.dma_start(
-                out=x_nat[c][:], in_=x[rows, :].rearrange("(p r) k -> p r k", r=4)
-            )
+            nc.sync.dma_start(out=x_nat[c][:], in_=chunk_rows(x, c))
 
         def load_h(c):
-            rows = slice(c * CHUNK, (c + 1) * CHUNK)
-            nc.sync.dma_start(
-                out=h_nat[c][:], in_=hidden[rows, :].rearrange("(p r) k -> p r k", r=4)
-            )
+            nc.sync.dma_start(out=h_nat[c][:], in_=chunk_rows(hidden, c))
 
         load_weight(win_nat, W_in_w)
         load_x(0)
@@ -110,8 +111,8 @@ def tile_liquidcell_pa_t_kernel(
                 nc.scalar.copy(out=dst, in_=src)
 
         def transpose_group(src_words, grouped, engines):
-            gw = grouped[:].bitcast(F32).rearrange("p (b u) -> p b u", u=2)
-            for half in range(2):
+            gw = grouped.bitcast(F32).rearrange("p (b u) -> p b u", u=2)
+            for half in range(src_words.shape[1] // 2):
                 bank = tp_psum.tile([P, 2, 256], F32, name="bank", tag="tp")
                 for j in range(2):
                     r = 2 * half + j
@@ -129,39 +130,39 @@ def tile_liquidcell_pa_t_kernel(
 
         def quantise(unit):
             grouped, codes, scales = unit
-            nc.vector.quantize_mx(
-                out=codes[:].bitcast(FP8X4), scales=scales[:], in_=grouped[:]
-            )
+            nc.vector.quantize_mx(out=codes.bitcast(FP8X4), scales=scales, in_=grouped)
 
         w_ops = {}
 
-        def weight_unit(o, g, src_words, engines):
+        def weight_unit(o, g, src, engines):
             gwt = grp.tile([P, 2048], BF16, name="gwt", tag="gw", align_bytes=64)
-            transpose_group(src_words, gwt, engines)
+            transpose_group(src[:].bitcast(F32), gwt[:], engines)
             codes = wq.tile([P, 512], U32, name="w_codes%d%d" % (o, g), align_bytes=64)
             scales = wq.tile([P, 512], U8, name="w_scales%d%d" % (o, g), align_bytes=64)
             w_ops[(o, g)] = (codes, scales)
-            return (gwt, codes, scales)
+            return (gwt[:], codes[:], scales[:])
 
         a_ops = {}
         g_hid = {}
 
         def x_unit(c, engines):
+            n = CHUNKS[c]
             gx = grp.tile([P, 2048], BF16, name="gx", tag="gx", align_bytes=64)
-            transpose_group(x_nat[c][:].bitcast(F32), gx, engines)
+            transpose_group(x_nat[c][:].bitcast(F32), gx[:, 0 : 4 * n], engines)
             xc = qp.tile([P, 512], U32, name="xc", tag="xc", align_bytes=64)
             xs = qp.tile([P, 512], U8, name="xs", tag="xs", align_bytes=64)
-            a_ops[(c, 0)] = (xc, xs)
-            return (gx, xc, xs)
+            a_ops[(c, 0)] = (xc[:, 0:n], xs[:, 0:n])
+            return (gx[:, 0 : 4 * n], xc[:, 0:n], xs[:, 0:n])
 
         def h_unit(c, engines):
+            n = CHUNKS[c]
             gh = grp.tile([P, 2048], BF16, name="gh", tag="gh", bufs=3, align_bytes=64)
-            transpose_group(h_nat[c][:].bitcast(F32), gh, engines)
+            transpose_group(h_nat[c][:].bitcast(F32), gh[:, 0 : 4 * n], engines)
             hc = qp.tile([P, 512], U32, name="hc", tag="hc", align_bytes=64)
             hs = qp.tile([P, 512], U8, name="hs", tag="hs", align_bytes=64)
-            a_ops[(c, 1)] = (hc, hs)
-            g_hid[c] = gh
-            return (gh, hc, hs)
+            a_ops[(c, 1)] = (hc[:, 0:n], hs[:, 0:n])
+            g_hid[c] = gh[:, 0 : 4 * n].rearrange("p (b t) -> p t b", t=4)
+            return (gh[:, 0 : 4 * n], hc[:, 0:n], hs[:, 0:n])
 
         a_tiles = {}
         v_tiles = {}
@@ -170,11 +171,11 @@ def tile_liquidcell_pa_t_kernel(
         def mm_pass(acc, c, o, g, t):
             cols = slice(t * P, (t + 1) * P)
             nc.tensor.matmul_mx(
-                out=acc[:],
+                out=acc[:, 0 : CHUNKS[c]],
                 lhsT=w_ops[(o, g)][0][:, cols].bitcast(FP8X4),
                 lhsT_scale=w_ops[(o, g)][1][:, cols],
-                rhs=a_ops[(c, g)][0][:].bitcast(FP8X4),
-                rhs_scale=a_ops[(c, g)][1][:],
+                rhs=a_ops[(c, g)][0].bitcast(FP8X4),
+                rhs_scale=a_ops[(c, g)][1],
                 start=(g == 0),
                 stop=(g == 1),
             )
@@ -184,18 +185,19 @@ def tile_liquidcell_pa_t_kernel(
             return acc
 
         def tanh_out(acc, c, o, t):
+            n = CHUNKS[c]
             if o == 0:
                 nc.scalar.activation(
-                    out=a_tiles[c][:, t, :], in_=acc[:], func=ACT.Tanh,
+                    out=a_tiles[c][:, t, 0:n], in_=acc[:, 0:n], func=ACT.Tanh,
                     bias=cst[:, t : t + 1], scale=1.0,
                 )
             else:
                 nc.scalar.activation(
-                    out=v_tiles[c][:, t, :], in_=acc[:], func=ACT.Tanh,
+                    out=v_tiles[c][:, t, 0:n], in_=acc[:, 0:n], func=ACT.Tanh,
                     bias=b_tau[:, t : t + 1], scale=0.5,
                 )
 
-        def new_elementwise(c, o):
+        def start_elementwise(c, o):
             if o == 0:
                 a_t = ep.tile([P, 4, 512], F32, name="a_t", tag="a_t", bufs=3)
                 a_tiles[c] = a_t
@@ -204,35 +206,47 @@ def tile_liquidcell_pa_t_kernel(
                 v_tiles[c] = v_t
 
         def matmuls(c, o):
-            new_elementwise(c, o)
+            start_elementwise(c, o)
             for t in range(4):
                 acc = new_acc()
                 for g in range(2):
                     mm_pass(acc, c, o, g, t)
                 tanh_out(acc, c, o, t)
 
-        def h_T(c):
-            return g_hid[c][:].rearrange("p (b t) -> p t b", t=4)
-
         def diff(c, ts, engine):
+            n = CHUNKS[c]
             engine.tensor_tensor(
-                out=a_tiles[c][:, ts, :], in0=a_tiles[c][:, ts, :],
-                in1=h_T(c)[:, ts, :], op=ALU.subtract,
+                out=a_tiles[c][:, ts, 0:n], in0=a_tiles[c][:, ts, 0:n],
+                in1=g_hid[c][:, ts, :], op=ALU.subtract,
             )
 
-        def weight_v(c, t, engine):
-            if engine == "s":
-                nc.scalar.activation(
-                    out=v_tiles[c][:, t, :], in_=v_tiles[c][:, t, :], func=ACT.Identity,
-                    bias=two_c[:, t : t + 1], scale=neg_c[:, t : t + 1],
-                )
-            else:
-                eng = nc.vector if engine == "v" else nc.gpsimd
-                eng.tensor_scalar(
-                    out=v_tiles[c][:, t, :], in0=v_tiles[c][:, t, :],
-                    scalar1=neg_c[:, t : t + 1], scalar2=two_c[:, t : t + 1],
-                    op0=ALU.mult, op1=ALU.add,
-                )
+        def weights(c, mine):
+            n = CHUNKS[c]
+            for t, engine in enumerate(W_ENGINES.get(c, "ssgg")):
+                if engine not in mine:
+                    continue
+                v_cols = v_tiles[c][:, t, 0:n]
+                mult, plus = neg_c[:, t : t + 1], two_c[:, t : t + 1]
+                if engine == "s":
+                    nc.scalar.activation(
+                        out=v_cols, in_=v_cols, func=ACT.Identity, bias=plus, scale=mult
+                    )
+                elif engine == "v":
+                    nc.vector.tensor_scalar(
+                        out=v_cols, in0=v_cols, scalar1=mult, scalar2=plus,
+                        op0=ALU.mult, op1=ALU.add,
+                    )
+                else:
+                    nc.gpsimd.tensor_scalar(
+                        out=v_cols, in0=v_cols, scalar1=mult, scalar2=plus,
+                        op0=ALU.mult, op1=ALU.add,
+                    )
+
+        gate = const.tile([P, 1], F32, name="gate")
+
+        def hold_gpsimd(c):
+            end = CHUNKS[c]
+            nc.gpsimd.tensor_copy(out=gate[:], in_=a_tiles[c][:, 3, end - 1 : end])
 
         def prod(c, cols):
             nc.vector.tensor_tensor(
@@ -240,16 +254,25 @@ def tile_liquidcell_pa_t_kernel(
                 in1=a_tiles[c][:, :, cols], op=ALU.mult,
             )
 
-        def prod_last(c, cols):
-            nc.vector.scalar_tensor_tensor(
-                out=v_tiles[c][:, :, cols], in0=v_tiles[c][:, :, cols], scalar=2.0,
-                in1=a_tiles[c][:, :, cols], op0=ALU.subtract, op1=ALU.mult,
-            )
-
+        last = N_CHUNKS - 1
         b_banks = {}
 
+        def back(c, r):
+            if c in (last - 1,):
+                bt = acc_psum.tile([P, 4, P], F32, name="bt_acc", tag="acc")
+            else:
+                bt = tp_psum.tile([P, 4, P], F32, name="bt", tag="tp")
+            for t in range(4):
+                nc.tensor.transpose(
+                    bt[:, t, :], v_tiles[c][:, t, r * P : (r + 1) * P], ident[:]
+                )
+            b_banks[(c, r)] = bt
+
         def back_h(c, r):
-            bt = tp_psum.tile([P, 4, P], F32, name="bt", tag="tp")
+            if c in (last - 1,):
+                bt = acc_psum.tile([P, 4, P], F32, name="bt_acc", tag="acc")
+            else:
+                bt = tp_psum.tile([P, 4, P], F32, name="bt", tag="tp")
             nc.tensor.matmul(
                 bt[:].rearrange("b t p -> b (t p)"), lhsT=ident_h[:],
                 rhs=h_nat[c][:, r, :].rearrange("b (u p e) -> b u e p", u=2, e=2),
@@ -264,144 +287,137 @@ def tile_liquidcell_pa_t_kernel(
                     rhs=ident[:], start=False, stop=(t == 3), is_transpose=True,
                 )
 
-        def back(c, r):
-            bt = tp_psum.tile([P, 4, P], F32, name="bt", tag="tp")
-            for t in range(4):
-                nc.tensor.transpose(
-                    bt[:, t, :], v_tiles[c][:, t, r * P : (r + 1) * P], ident[:]
-                )
-            b_banks[(c, r)] = bt
-
-        def o_tile(c):
+        def o_rows(c, r):
             if c not in o_tiles:
-                o_sb = ep.tile([P, 4, 512], F32, name="o_sb", tag="o_sb")
+                o_sb = ep.tile([P, 4, 512], F32, name="o_sb", tag="o_sb", bufs=2)
                 o_tiles[c] = o_sb
-            return o_tiles[c]
+            return o_tiles[c][:, r, :].rearrange("b (u p e) -> b u p e", u=2, e=2)
 
         def finish(c, r):
             nc.vector.tensor_tensor(
-                out=o_tile(c)[:, r, :].rearrange("b (u p e) -> b u p e", u=2, e=2),
+                out=o_rows(c, r),
                 in0=b_banks[(c, r)][:].rearrange("b (u e) p -> b u p e", u=2),
                 in1=h_nat[c][:, r, :].rearrange("b (u p e) -> b u p e", u=2, e=2),
                 op=ALU.add,
             )
 
-        def finish_s(c, r, engine):
+        def finish_copy(c, r, engine):
             copy_on(
-                engine,
-                o_tile(c)[:, r, :].rearrange("b (u p e) -> b u p e", u=2, e=2),
+                engine, o_rows(c, r),
                 b_banks[(c, r)][:].rearrange("b (u e) p -> b u p e", u=2),
             )
 
         def store(c, r0, r1):
             nc.sync.dma_start(
-                out=out[c * CHUNK : (c + 1) * CHUNK, :].rearrange(
-                    "(p r) h -> p r h", r=4
-                )[:, r0:r1, :],
-                in_=o_tiles[c][:, r0:r1, :],
+                out=chunk_rows(out, c)[:, r0:r1, :], in_=o_tiles[c][:, r0:r1, :]
             )
 
-        ALL = slice(0, 512)
         VS = ("v", "s")
         SS = ("s", "s")
+        W_ENGINES = {0: "vvvv", last: "ssss"}
+        ON_PE = {last - 1: 2}
 
-        u0 = weight_unit(0, 0, win_nat[:].bitcast(F32), VS)
+        def n_rows(c):
+            return CHUNKS[c] // P
+
+        def on_vector(c):
+            return range(n_rows(c) - ON_PE.get(c, 0))
+
+        def on_scalar(c):
+            return range(n_rows(c) - ON_PE.get(c, 0), n_rows(c))
+
+        u0 = weight_unit(0, 0, win_nat, VS)
         u1 = x_unit(0, VS)
         quantise(u0)
-        u2 = weight_unit(0, 1, wrec_nat[:].bitcast(F32), VS)
         quantise(u1)
-        u3 = h_unit(0, VS)
+        u2 = weight_unit(0, 1, wrec_nat, VS)
         quantise(u2)
-        u4 = weight_unit(1, 0, wtx_nat[:].bitcast(F32), VS)
+        u3 = h_unit(0, VS)
         quantise(u3)
-
         vt = tp_psum.tile([P, 2, 256], F32, name="vt", tag="tp")
         nc.tensor.transpose(vt[:, 0, 0:P], vec_rows[:].bitcast(F32), ident[:])
         cst = const.tile([P, 12], F32, name="cst")
-        nc.vector.tensor_copy(
+        nc.scalar.copy(
             out=cst[:], in_=vt[:].rearrange("p u b -> p (u b)").bitcast(BF16)[:, 0:12]
         )
         b_tau = const.tile([P, 4], F32, name="b_tau")
-        nc.vector.tensor_scalar(
+        nc.gpsimd.tensor_scalar(
             out=b_tau[:], in0=cst[:, 8:12], scalar1=0.5, scalar2=0.5 * math.log(3.0),
             op0=ALU.mult, op1=ALU.add,
         )
-        inv_tb = const.tile([P, 4], F32, name="inv_tb")
-        nc.vector.reciprocal(out=inv_tb[:], in_=cst[:, 4:8])
-        neg_c = const.tile([P, 4], F32, name="neg_c")
-        nc.vector.tensor_scalar_mul(out=neg_c[:], in0=inv_tb[:], scalar1=-1.0 / 15.0)
-        two_c = const.tile([P, 4], F32, name="two_c")
-        nc.vector.tensor_scalar_mul(out=two_c[:], in0=inv_tb[:], scalar1=2.0 / 15.0)
-
-        new_elementwise(0, 0)
+        start_elementwise(0, 0)
         acc0 = [new_acc(), new_acc(), new_acc(), new_acc()]
         for t in range(4):
             mm_pass(acc0[t], 0, 0, 0, t)
-        u5 = weight_unit(1, 1, wth_nat[:].bitcast(F32), VS)
+        u4 = weight_unit(1, 0, wtx_nat, VS)
+        u5 = weight_unit(1, 1, wth_nat, VS)
         for t in range(4):
             mm_pass(acc0[t], 0, 0, 1, t)
             tanh_out(acc0[t], 0, 0, t)
         quantise(u4)
         quantise(u5)
-        u6 = x_unit(1, ("v", "v"))
-        u7 = h_unit(1, ("v", "s"))
+        inv_tb = const.tile([P, 4], F32, name="inv_tb")
+        nc.vector.reciprocal(out=inv_tb[:], in_=cst[:, 4:8])
+        neg_c = const.tile([P, 4], F32, name="neg_c")
+        nc.gpsimd.tensor_scalar(
+            out=neg_c[:], in0=inv_tb[:], scalar1=-1.0 / 15.0, scalar2=0.0,
+            op0=ALU.mult, op1=ALU.add,
+        )
+        two_c = const.tile([P, 4], F32, name="two_c")
+        nc.gpsimd.tensor_scalar(
+            out=two_c[:], in0=inv_tb[:], scalar1=2.0 / 15.0, scalar2=0.0,
+            op0=ALU.mult, op1=ALU.add,
+        )
+        u6 = x_unit(1, "vv")
+        u7 = h_unit(1, "vs")
         quantise(u6)
         quantise(u7)
         matmuls(0, 1)
         diff(0, slice(0, 4), nc.vector)
 
-        def weights(c, engines):
-            for t in range(4):
-                weight_v(c, t, engines[t])
+        weights(0, "sg")
 
-        weights(0, ("s", "s", "v", "v"))
-        last = N_CHUNKS - 1
-        K = 0
-        D3 = False
         for c in range(1, N_CHUNKS):
-            more = c + 1 < N_CHUNKS
+            more = c < last
             if c >= 2:
-                for r in range(4):
-                    if r < 4 - K:
-                        finish(c - 2, r)
+                for r in on_vector(c - 2):
+                    finish(c - 2, r)
             matmuls(c, 0)
             if c >= 2:
-                for r in range(4 - K, 4):
-                    finish_s(c - 2, r, "s")
-                store(c - 2, 0, 4)
+                for r in on_scalar(c - 2):
+                    finish_copy(c - 2, r, "s")
+                store(c - 2, 0, n_rows(c - 2))
             if more:
                 ux = x_unit(c + 1, SS)
                 uh = h_unit(c + 1, SS)
-            prod(c - 1, ALL)
+            weights(c - 1, "v")
+            prod(c - 1, slice(0, CHUNKS[c - 1]))
             matmuls(c, 1)
             if more:
-                weights(c, ("s", "s", "g", "g"))
+                weights(c, "s")
                 quantise(ux)
                 quantise(uh)
-            if D3 and more:
-                diff(c, slice(0, 3), nc.vector)
-                diff(c, slice(3, 4), nc.gpsimd)
+            diff(c, slice(0, 4), nc.vector)
+            if more:
+                hold_gpsimd(c)
+                weights(c, "g")
             else:
-                diff(c, slice(0, 4), nc.vector)
-            if not more:
-                weights(c, ("s", "s", "s", "s"))
-            for r in range(4):
-                if r < 4 - K - (c == last) * 2:
-                    back(c - 1, r)
-                else:
-                    back_h(c - 1, r)
-                    back_p(c - 1, r)
+                weights(c, "s")
+            for r in on_vector(c - 1):
+                back(c - 1, r)
+            for r in on_scalar(c - 1):
+                back_h(c - 1, r)
+                back_p(c - 1, r)
 
-        for r in range(4):
-            if r < 4 - K - 2:
-                finish(last - 1, r)
-            else:
-                finish_s(last - 1, r, "s")
-        store(last - 1, 0, 4)
-        for r in range(4):
+        for r in on_vector(last - 1):
+            finish(last - 1, r)
+        for r in on_scalar(last - 1):
+            finish_copy(last - 1, r, "s")
+        store(last - 1, 0, n_rows(last - 1))
+        weights(last, "v")
+        for r in range(n_rows(last)):
             back_h(last, r)
-        for r in range(4):
             prod(last, slice(r * P, (r + 1) * P))
             back_p(last, r)
-            finish_s(last, r, "s")
+            finish_copy(last, r, "v" if r == n_rows(last) - 1 else "s")
             store(last, r, r + 1)

@@ -30,8 +30,7 @@ def tile_liquidcell_pa_t_kernel(
         grp = ctx.enter_context(tc.tile_pool(name="grp", bufs=2))
         qp = ctx.enter_context(tc.tile_pool(name="qp", bufs=2))
         ep = ctx.enter_context(tc.tile_pool(name="ep", bufs=2))
-        tp_psum = ctx.enter_context(tc.psum_pool(name="tp_psum", bufs=4))
-        acc_psum = ctx.enter_context(tc.psum_pool(name="acc_psum", bufs=4))
+        psum = ctx.enter_context(tc.psum_pool(name="psum", bufs=8))
         ctx.enter_context(tc.manual_schedule())
 
         warm = const.tile([P, 1], F32, name="warm")
@@ -100,9 +99,20 @@ def tile_liquidcell_pa_t_kernel(
             load_tau_rows(wtx_nat, u, slice(0, I))
         for u in range(2):
             load_tau_rows(wth_nat, u, slice(I, I + H))
-        for c in range(1, N_CHUNKS):
-            load_x(c)
-            load_h(c)
+        load_x(1)
+        load_h(1)
+        load_x(2)
+        load_h(2)
+        load_x(3)
+        load_h(3)
+        load_x(4)
+        load_h(4)
+        load_x(5)
+        load_h(5)
+        load_x(6)
+        load_h(6)
+        load_x(7)
+        load_h(7)
 
         def copy_on(engine, dst, src):
             if engine == "v":
@@ -110,169 +120,148 @@ def tile_liquidcell_pa_t_kernel(
             else:
                 nc.scalar.copy(out=dst, in_=src)
 
-        def transpose_group(src_words, grouped, engines):
-            gw = grouped.bitcast(F32).rearrange("p (b u) -> p b u", u=2)
-            for half in range(src_words.shape[1] // 2):
-                bank = tp_psum.tile([P, 2, 256], F32, name="bank", tag="tp")
+        units = {}
+        ops = {}
+        g_hid = {}
+        banks = {}
+
+        def tr(k, c):
+            n = 512 if k in ("win", "wrec", "wtx", "wth") else CHUNKS[c]
+            src = {"win": win_nat, "wrec": wrec_nat, "wtx": wtx_nat, "wth": wth_nat}.get(k)
+            if k == "x":
+                src = x_nat[c]
+            if k == "h":
+                src = h_nat[c]
+            words = src[:].bitcast(F32)
+            for half in range(n // 256):
+                bank = psum.tile([P, 2, 256], F32, name="bank", tag="ps")
                 for j in range(2):
-                    r = 2 * half + j
                     for u in range(2):
                         nc.tensor.transpose(
                             bank[:, u, j * P : (j + 1) * P],
-                            src_words[:, r, u * P : (u + 1) * P],
-                            ident[:],
+                            words[:, 2 * half + j, u * P : (u + 1) * P], ident[:],
                         )
-                copy_on(
-                    engines[half],
-                    gw[:, half * 256 : (half + 1) * 256, :],
-                    bank[:].rearrange("p u b -> p b u"),
-                )
+                banks[(k, c, half)] = bank
+            if k == "x":
+                g = grp.tile([P, 2048], BF16, name="gx", tag="gx", bufs=3, align_bytes=64)
+                codes = qp.tile([P, 512], U32, name="xc", tag="xc", bufs=3, align_bytes=64)
+                scales = qp.tile([P, 512], U8, name="xs", tag="xs", bufs=3, align_bytes=64)
+            elif k == "h":
+                g = grp.tile([P, 2048], BF16, name="gh", tag="gh", bufs=4, align_bytes=64)
+                codes = qp.tile([P, 512], U32, name="hc", tag="hc", bufs=3, align_bytes=64)
+                scales = qp.tile([P, 512], U8, name="hs", tag="hs", bufs=3, align_bytes=64)
+                g_hid[c] = g[:, 0 : 4 * n].rearrange("p (b t) -> p t b", t=4)
+            else:
+                g = grp.tile([P, 2048], BF16, name="gw", tag="gw", bufs=3, align_bytes=64)
+                codes = wq.tile([P, 512], U32, name="w_codes" + k, align_bytes=64)
+                scales = wq.tile([P, 512], U8, name="w_scales" + k, align_bytes=64)
+            units[(k, c)] = (g[:, 0 : 4 * n], codes[:, 0:n], scales[:, 0:n])
 
-        def quantise(unit):
-            grouped, codes, scales = unit
-            nc.vector.quantize_mx(out=codes.bitcast(FP8X4), scales=scales, in_=grouped)
+        def cp(k, c, half, engine):
+            gw = units[(k, c)][0].bitcast(F32).rearrange("p (b u) -> p b u", u=2)
+            copy_on(
+                engine, gw[:, half * 256 : (half + 1) * 256, :],
+                banks[(k, c, half)][:].rearrange("p u b -> p b u"),
+            )
 
-        w_ops = {}
-
-        def weight_unit(o, g, src, engines):
-            gwt = grp.tile([P, 2048], BF16, name="gwt", tag="gw", align_bytes=64)
-            transpose_group(src[:].bitcast(F32), gwt[:], engines)
-            codes = wq.tile([P, 512], U32, name="w_codes%d%d" % (o, g), align_bytes=64)
-            scales = wq.tile([P, 512], U8, name="w_scales%d%d" % (o, g), align_bytes=64)
-            w_ops[(o, g)] = (codes, scales)
-            return (gwt[:], codes[:], scales[:])
-
-        a_ops = {}
-        g_hid = {}
-
-        def x_unit(c, engines):
-            n = CHUNKS[c]
-            gx = grp.tile([P, 2048], BF16, name="gx", tag="gx", align_bytes=64)
-            transpose_group(x_nat[c][:].bitcast(F32), gx[:, 0 : 4 * n], engines)
-            xc = qp.tile([P, 512], U32, name="xc", tag="xc", align_bytes=64)
-            xs = qp.tile([P, 512], U8, name="xs", tag="xs", align_bytes=64)
-            a_ops[(c, 0)] = (xc[:, 0:n], xs[:, 0:n])
-            return (gx[:, 0 : 4 * n], xc[:, 0:n], xs[:, 0:n])
-
-        def h_unit(c, engines):
-            n = CHUNKS[c]
-            gh = grp.tile([P, 2048], BF16, name="gh", tag="gh", bufs=3, align_bytes=64)
-            transpose_group(h_nat[c][:].bitcast(F32), gh[:, 0 : 4 * n], engines)
-            hc = qp.tile([P, 512], U32, name="hc", tag="hc", align_bytes=64)
-            hs = qp.tile([P, 512], U8, name="hs", tag="hs", align_bytes=64)
-            a_ops[(c, 1)] = (hc[:, 0:n], hs[:, 0:n])
-            g_hid[c] = gh[:, 0 : 4 * n].rearrange("p (b t) -> p t b", t=4)
-            return (gh[:, 0 : 4 * n], hc[:, 0:n], hs[:, 0:n])
+        def q(k, c):
+            g, codes, scales = units[(k, c)]
+            nc.vector.quantize_mx(out=codes.bitcast(FP8X4), scales=scales, in_=g)
 
         a_tiles = {}
         v_tiles = {}
         o_tiles = {}
+        accs = {}
+        W = {(0, 0): "win", (0, 1): "wrec", (1, 0): "wtx", (1, 1): "wth"}
 
-        def mm_pass(acc, c, o, g, t):
+        def mp(c, o, g, t):
             cols = slice(t * P, (t + 1) * P)
+            if (c, o, t) not in accs:
+                acc = psum.tile([P, 512], F32, name="acc", tag="ps")
+                accs[(c, o, t)] = acc
+            w = units[(W[(o, g)], 0)]
+            a = units[("xh"[g], c)]
             nc.tensor.matmul_mx(
-                out=acc[:, 0 : CHUNKS[c]],
-                lhsT=w_ops[(o, g)][0][:, cols].bitcast(FP8X4),
-                lhsT_scale=w_ops[(o, g)][1][:, cols],
-                rhs=a_ops[(c, g)][0].bitcast(FP8X4),
-                rhs_scale=a_ops[(c, g)][1],
-                start=(g == 0),
-                stop=(g == 1),
+                out=accs[(c, o, t)][:, 0 : CHUNKS[c]],
+                lhsT=w[1][:, cols].bitcast(FP8X4), lhsT_scale=w[2][:, cols],
+                rhs=a[1].bitcast(FP8X4), rhs_scale=a[2],
+                start=(g == 0), stop=(g == 1),
             )
 
-        def new_acc():
-            acc = acc_psum.tile([P, 512], F32, name="acc", tag="acc")
-            return acc
-
-        def tanh_out(acc, c, o, t):
-            n = CHUNKS[c]
-            if o == 0:
-                nc.scalar.activation(
-                    out=a_tiles[c][:, t, 0:n], in_=acc[:, 0:n], func=ACT.Tanh,
-                    bias=cst[:, t : t + 1], scale=1.0,
-                )
-            else:
-                nc.scalar.activation(
-                    out=v_tiles[c][:, t, 0:n], in_=acc[:, 0:n], func=ACT.Tanh,
-                    bias=b_tau[:, t : t + 1], scale=0.5,
-                )
-
-        def start_elementwise(c, o):
-            if o == 0:
-                a_t = ep.tile([P, 4, 512], F32, name="a_t", tag="a_t", bufs=3)
-                a_tiles[c] = a_t
-            else:
-                v_t = ep.tile([P, 4, 512], F32, name="v_t", tag="v_t", bufs=3)
-                v_tiles[c] = v_t
-
-        def matmuls(c, o):
-            start_elementwise(c, o)
+        def mg(c, o, g):
             for t in range(4):
-                acc = new_acc()
-                for g in range(2):
-                    mm_pass(acc, c, o, g, t)
-                tanh_out(acc, c, o, t)
+                mp(c, o, g, t)
 
-        def diff(c, ts, engine):
+        def mt(c, o, t):
+            mp(c, o, 0, t)
+            mp(c, o, 1, t)
+
+        def th(c, o, t):
             n = CHUNKS[c]
-            engine.tensor_tensor(
-                out=a_tiles[c][:, ts, 0:n], in0=a_tiles[c][:, ts, 0:n],
-                in1=g_hid[c][:, ts, :], op=ALU.subtract,
+            tiles = (a_tiles, v_tiles)[o]
+            if c not in tiles:
+                if o == 0:
+                    a_t = ep.tile([P, 4, 512], F32, name="a_t", tag="a_t", bufs=3)
+                    tiles[c] = a_t
+                else:
+                    v_t = ep.tile([P, 4, 512], F32, name="v_t", tag="v_t", bufs=3)
+                    tiles[c] = v_t
+            nc.scalar.activation(
+                out=tiles[c][:, t, 0:n], in_=accs[(c, o, t)][:, 0:n], func=ACT.Tanh,
+                bias=(cst, b_tau)[o][:, t : t + 1], scale=(1.0, 0.5)[o],
             )
 
-        def weights(c, mine):
+        def ms(c, o):
+            for t in range(4):
+                mt(c, o, t)
+                th(c, o, t)
+
+        def df(c):
             n = CHUNKS[c]
-            for t, engine in enumerate(W_ENGINES.get(c, "ssgg")):
-                if engine not in mine:
-                    continue
+            nc.vector.tensor_tensor(
+                out=a_tiles[c][:, :, 0:n], in0=a_tiles[c][:, :, 0:n], in1=g_hid[c], op=ALU.subtract
+            )
+
+        def wt(c, ts, engine):
+            n = CHUNKS[c]
+            for t in ts:
                 v_cols = v_tiles[c][:, t, 0:n]
                 mult, plus = neg_c[:, t : t + 1], two_c[:, t : t + 1]
                 if engine == "s":
                     nc.scalar.activation(
                         out=v_cols, in_=v_cols, func=ACT.Identity, bias=plus, scale=mult
                     )
-                elif engine == "v":
-                    nc.vector.tensor_scalar(
-                        out=v_cols, in0=v_cols, scalar1=mult, scalar2=plus,
-                        op0=ALU.mult, op1=ALU.add,
-                    )
                 else:
-                    nc.gpsimd.tensor_scalar(
+                    (nc.vector if engine == "v" else nc.gpsimd).tensor_scalar(
                         out=v_cols, in0=v_cols, scalar1=mult, scalar2=plus,
                         op0=ALU.mult, op1=ALU.add,
                     )
 
-        gate = const.tile([P, 1], F32, name="gate")
-
-        def hold_gpsimd(c):
-            end = CHUNKS[c]
-            nc.gpsimd.tensor_copy(out=gate[:], in_=a_tiles[c][:, 3, end - 1 : end])
-
-        def prod(c, cols):
+        def pr(c, r0, r1):
+            cols = slice(r0 * P, r1 * P)
             nc.vector.tensor_tensor(
                 out=v_tiles[c][:, :, cols], in0=v_tiles[c][:, :, cols],
                 in1=a_tiles[c][:, :, cols], op=ALU.mult,
             )
 
-        last = N_CHUNKS - 1
         b_banks = {}
 
-        def back(c, r):
-            if c in (last - 1,):
-                bt = acc_psum.tile([P, 4, P], F32, name="bt_acc", tag="acc")
+        def bk(c, r, pool="t"):
+            if pool == "t":
+                bt = psum.tile([P, 4, P], F32, name="bt", tag="ps")
             else:
-                bt = tp_psum.tile([P, 4, P], F32, name="bt", tag="tp")
+                bt = psum.tile([P, 4, P], F32, name="bta", tag="ps")
             for t in range(4):
                 nc.tensor.transpose(
                     bt[:, t, :], v_tiles[c][:, t, r * P : (r + 1) * P], ident[:]
                 )
             b_banks[(c, r)] = bt
 
-        def back_h(c, r):
-            if c in (last - 1,):
-                bt = acc_psum.tile([P, 4, P], F32, name="bt_acc", tag="acc")
+        def bh(c, r, pool="t"):
+            if pool == "t":
+                bt = psum.tile([P, 4, P], F32, name="bt", tag="ps")
             else:
-                bt = tp_psum.tile([P, 4, P], F32, name="bt", tag="tp")
+                bt = psum.tile([P, 4, P], F32, name="bta", tag="ps")
             nc.tensor.matmul(
                 bt[:].rearrange("b t p -> b (t p)"), lhsT=ident_h[:],
                 rhs=h_nat[c][:, r, :].rearrange("b (u p e) -> b u e p", u=2, e=2),
@@ -280,7 +269,7 @@ def tile_liquidcell_pa_t_kernel(
             )
             b_banks[(c, r)] = bt
 
-        def back_p(c, r):
+        def bp(c, r):
             for t in range(4):
                 nc.tensor.matmul(
                     b_banks[(c, r)][:, t, :], lhsT=v_tiles[c][:, t, r * P : (r + 1) * P],
@@ -293,7 +282,7 @@ def tile_liquidcell_pa_t_kernel(
                 o_tiles[c] = o_sb
             return o_tiles[c][:, r, :].rearrange("b (u p e) -> b u p e", u=2, e=2)
 
-        def finish(c, r):
+        def fa(c, r):
             nc.vector.tensor_tensor(
                 out=o_rows(c, r),
                 in0=b_banks[(c, r)][:].rearrange("b (u e) p -> b u p e", u=2),
@@ -301,123 +290,259 @@ def tile_liquidcell_pa_t_kernel(
                 op=ALU.add,
             )
 
-        def finish_copy(c, r, engine):
+        def fc(c, r, engine):
             copy_on(
                 engine, o_rows(c, r),
                 b_banks[(c, r)][:].rearrange("b (u e) p -> b u p e", u=2),
             )
 
-        def store(c, r0, r1):
+        def st(c, r0, r1):
             nc.sync.dma_start(
                 out=chunk_rows(out, c)[:, r0:r1, :], in_=o_tiles[c][:, r0:r1, :]
             )
 
-        VS = ("v", "s")
-        SS = ("s", "s")
-        W_ENGINES = {0: "vvvv", last: "ssss"}
-        ON_PE = {last - 1: 2}
-
-        def n_rows(c):
-            return CHUNKS[c] // P
-
-        def on_vector(c):
-            return range(n_rows(c) - ON_PE.get(c, 0))
-
-        def on_scalar(c):
-            return range(n_rows(c) - ON_PE.get(c, 0), n_rows(c))
-
-        u0 = weight_unit(0, 0, win_nat, VS)
-        u1 = x_unit(0, VS)
-        quantise(u0)
-        quantise(u1)
-        u2 = weight_unit(0, 1, wrec_nat, VS)
-        quantise(u2)
-        u3 = h_unit(0, VS)
-        quantise(u3)
-        vt = tp_psum.tile([P, 2, 256], F32, name="vt", tag="tp")
-        nc.tensor.transpose(vt[:, 0, 0:P], vec_rows[:].bitcast(F32), ident[:])
         cst = const.tile([P, 12], F32, name="cst")
-        nc.scalar.copy(
-            out=cst[:], in_=vt[:].rearrange("p u b -> p (u b)").bitcast(BF16)[:, 0:12]
-        )
         b_tau = const.tile([P, 4], F32, name="b_tau")
-        nc.gpsimd.tensor_scalar(
-            out=b_tau[:], in0=cst[:, 8:12], scalar1=0.5, scalar2=0.5 * math.log(3.0),
-            op0=ALU.mult, op1=ALU.add,
-        )
-        start_elementwise(0, 0)
-        acc0 = [new_acc(), new_acc(), new_acc(), new_acc()]
-        for t in range(4):
-            mm_pass(acc0[t], 0, 0, 0, t)
-        u4 = weight_unit(1, 0, wtx_nat, VS)
-        u5 = weight_unit(1, 1, wth_nat, VS)
-        for t in range(4):
-            mm_pass(acc0[t], 0, 0, 1, t)
-            tanh_out(acc0[t], 0, 0, t)
-        quantise(u4)
-        quantise(u5)
         inv_tb = const.tile([P, 4], F32, name="inv_tb")
-        nc.vector.reciprocal(out=inv_tb[:], in_=cst[:, 4:8])
         neg_c = const.tile([P, 4], F32, name="neg_c")
-        nc.gpsimd.tensor_scalar(
-            out=neg_c[:], in0=inv_tb[:], scalar1=-1.0 / 15.0, scalar2=0.0,
-            op0=ALU.mult, op1=ALU.add,
-        )
         two_c = const.tile([P, 4], F32, name="two_c")
-        nc.gpsimd.tensor_scalar(
-            out=two_c[:], in0=inv_tb[:], scalar1=2.0 / 15.0, scalar2=0.0,
-            op0=ALU.mult, op1=ALU.add,
-        )
-        u6 = x_unit(1, "vv")
-        u7 = h_unit(1, "vs")
-        quantise(u6)
-        quantise(u7)
-        matmuls(0, 1)
-        diff(0, slice(0, 4), nc.vector)
 
-        weights(0, "sg")
+        def constants():
+            vt = psum.tile([P, 2, 256], F32, name="vt", tag="ps")
+            nc.tensor.transpose(vt[:, 0, 0:P], vec_rows[:].bitcast(F32), ident[:])
+            nc.scalar.copy(
+                out=cst[:], in_=vt[:].rearrange("p u b -> p (u b)").bitcast(BF16)[:, 0:12]
+            )
+            nc.gpsimd.tensor_scalar(
+                out=b_tau[:], in0=cst[:, 8:12], scalar1=0.5, scalar2=0.5 * math.log(3.0),
+                op0=ALU.mult, op1=ALU.add,
+            )
 
-        for c in range(1, N_CHUNKS):
-            more = c < last
-            if c >= 2:
-                for r in on_vector(c - 2):
-                    finish(c - 2, r)
-            matmuls(c, 0)
-            if c >= 2:
-                for r in on_scalar(c - 2):
-                    finish_copy(c - 2, r, "s")
-                store(c - 2, 0, n_rows(c - 2))
-            if more:
-                ux = x_unit(c + 1, SS)
-                uh = h_unit(c + 1, SS)
-            weights(c - 1, "v")
-            prod(c - 1, slice(0, CHUNKS[c - 1]))
-            matmuls(c, 1)
-            if more:
-                weights(c, "s")
-                quantise(ux)
-                quantise(uh)
-            diff(c, slice(0, 4), nc.vector)
-            if more:
-                hold_gpsimd(c)
-                weights(c, "g")
-            else:
-                weights(c, "s")
-            for r in on_vector(c - 1):
-                back(c - 1, r)
-            for r in on_scalar(c - 1):
-                back_h(c - 1, r)
-                back_p(c - 1, r)
+        def factors():
+            nc.vector.reciprocal(out=inv_tb[:], in_=cst[:, 4:8])
+            nc.gpsimd.tensor_scalar(
+                out=neg_c[:], in0=inv_tb[:], scalar1=-1.0 / 15.0, scalar2=0.0,
+                op0=ALU.mult, op1=ALU.add,
+            )
+            nc.gpsimd.tensor_scalar(
+                out=two_c[:], in0=inv_tb[:], scalar1=2.0 / 15.0, scalar2=0.0,
+                op0=ALU.mult, op1=ALU.add,
+            )
 
-        for r in on_vector(last - 1):
-            finish(last - 1, r)
-        for r in on_scalar(last - 1):
-            finish_copy(last - 1, r, "s")
-        store(last - 1, 0, n_rows(last - 1))
-        weights(last, "v")
-        for r in range(n_rows(last)):
-            back_h(last, r)
-            prod(last, slice(r * P, (r + 1) * P))
-            back_p(last, r)
-            finish_copy(last, r, "v" if r == n_rows(last) - 1 else "s")
-            store(last, r, r + 1)
+        tr("win", 0)
+        cp("win", 0, 0, "v")
+        cp("win", 0, 1, "s")
+        tr("x", 0)
+        cp("x", 0, 0, "v")
+        cp("x", 0, 1, "s")
+        q("win", 0)
+        q("x", 0)
+        tr("wrec", 0)
+        cp("wrec", 0, 0, "v")
+        cp("wrec", 0, 1, "s")
+        q("wrec", 0)
+        tr("h", 0)
+        cp("h", 0, 0, "s")
+        cp("h", 0, 1, "s")
+        q("h", 0)
+        constants()
+        mg(0, 0, 0)
+        tr("wtx", 0)
+        cp("wtx", 0, 0, "s")
+        cp("wtx", 0, 1, "s")
+        tr("wth", 0)
+        cp("wth", 0, 0, "v")
+        cp("wth", 0, 1, "s")
+        mg(0, 0, 1)
+        th(0, 0, 0)
+        th(0, 0, 1)
+        th(0, 0, 2)
+        th(0, 0, 3)
+        q("wtx", 0)
+        q("wth", 0)
+        factors()
+        tr("x", 1)
+        cp("x", 1, 0, "v")
+        cp("x", 1, 1, "v")
+        tr("h", 1)
+        cp("h", 1, 0, "v")
+        cp("h", 1, 1, "s")
+        q("x", 1)
+        q("h", 1)
+        ms(0, 1)
+        tr("x", 2)
+        cp("x", 2, 0, "s")
+        cp("x", 2, 1, "s")
+        tr("h", 2)
+        cp("h", 2, 0, "s")
+        cp("h", 2, 1, "s")
+        df(0)
+        wt(0, (0, 1, 2, 3,), "v")
+        pr(0, 0, 4)
+        q("x", 2)
+        q("h", 2)
+        ms(1, 0)
+        ms(1, 1)
+        tr("x", 3)
+        cp("x", 3, 0, "s")
+        cp("x", 3, 1, "s")
+        tr("h", 3)
+        cp("h", 3, 0, "s")
+        cp("h", 3, 1, "s")
+        bk(0, 0)
+        bk(0, 1)
+        bk(0, 2)
+        bk(0, 3)
+        wt(1, (0, 1,), "s")
+        df(1)
+        wt(1, (2, 3,), "g")
+        fa(0, 0)
+        fa(0, 1)
+        fa(0, 2)
+        fa(0, 3)
+        st(0, 0, 4)
+        pr(1, 0, 4)
+        q("x", 3)
+        q("h", 3)
+        ms(2, 0)
+        ms(2, 1)
+        tr("x", 4)
+        cp("x", 4, 0, "s")
+        cp("x", 4, 1, "s")
+        tr("h", 4)
+        cp("h", 4, 0, "s")
+        cp("h", 4, 1, "s")
+        bk(1, 0)
+        bk(1, 1)
+        bk(1, 2)
+        bk(1, 3)
+        wt(2, (0, 1,), "s")
+        df(2)
+        wt(2, (2, 3,), "g")
+        fa(1, 0)
+        fa(1, 1)
+        fa(1, 2)
+        fa(1, 3)
+        st(1, 0, 4)
+        pr(2, 0, 4)
+        q("x", 4)
+        q("h", 4)
+        ms(3, 0)
+        ms(3, 1)
+        tr("x", 5)
+        cp("x", 5, 0, "s")
+        cp("x", 5, 1, "s")
+        tr("h", 5)
+        cp("h", 5, 0, "s")
+        cp("h", 5, 1, "s")
+        bk(2, 0)
+        bk(2, 1)
+        bk(2, 2)
+        bk(2, 3)
+        wt(3, (0, 1,), "s")
+        df(3)
+        wt(3, (2, 3,), "g")
+        fa(2, 0)
+        fa(2, 1)
+        fa(2, 2)
+        fa(2, 3)
+        st(2, 0, 4)
+        pr(3, 0, 4)
+        q("x", 5)
+        q("h", 5)
+        ms(4, 0)
+        ms(4, 1)
+        tr("x", 6)
+        cp("x", 6, 0, "s")
+        cp("x", 6, 1, "s")
+        tr("h", 6)
+        cp("h", 6, 0, "s")
+        cp("h", 6, 1, "s")
+        bk(3, 0)
+        bk(3, 1)
+        bk(3, 2)
+        bk(3, 3)
+        wt(4, (0, 1,), "s")
+        df(4)
+        wt(4, (2, 3,), "g")
+        fa(3, 0)
+        fa(3, 1)
+        fa(3, 2)
+        fa(3, 3)
+        st(3, 0, 4)
+        pr(4, 0, 4)
+        q("x", 6)
+        q("h", 6)
+        ms(5, 0)
+        ms(5, 1)
+        tr("x", 7)
+        cp("x", 7, 0, "s")
+        cp("x", 7, 1, "s")
+        tr("h", 7)
+        cp("h", 7, 0, "s")
+        cp("h", 7, 1, "s")
+        bk(4, 0)
+        bk(4, 1)
+        bk(4, 2)
+        bk(4, 3)
+        wt(5, (0, 1,), "s")
+        df(5)
+        wt(5, (2, 3,), "g")
+        fa(4, 0)
+        fa(4, 1)
+        fa(4, 2)
+        fa(4, 3)
+        st(4, 0, 4)
+        pr(5, 0, 4)
+        q("x", 7)
+        q("h", 7)
+        ms(6, 0)
+        ms(6, 1)
+        bk(5, 0)
+        bk(5, 1)
+        bk(5, 2)
+        bk(5, 3)
+        wt(6, (0, 1,), "s")
+        df(6)
+        wt(6, (2, 3,), "g")
+        fa(5, 0)
+        fa(5, 1)
+        fa(5, 2)
+        fa(5, 3)
+        st(5, 0, 4)
+        pr(6, 0, 4)
+        ms(7, 0)
+        ms(7, 1)
+        bk(6, 0)
+        bk(6, 1)
+        bh(6, 2)
+        bp(6, 2)
+        bh(6, 3)
+        bp(6, 3)
+        wt(7, (0, 1, 2, 3,), "s")
+        df(7)
+        fa(6, 0)
+        fa(6, 1)
+        fc(6, 2, "s")
+        fc(6, 3, "s")
+        st(6, 0, 4)
+        bh(7, 0)
+        pr(7, 0, 1)
+        bp(7, 0)
+        fc(7, 0, "s")
+        st(7, 0, 1)
+        bh(7, 1)
+        pr(7, 1, 2)
+        bp(7, 1)
+        fc(7, 1, "s")
+        st(7, 1, 2)
+        bh(7, 2)
+        pr(7, 2, 3)
+        bp(7, 2)
+        fc(7, 2, "s")
+        st(7, 2, 3)
+        bh(7, 3)
+        pr(7, 3, 4)
+        bp(7, 3)
+        fc(7, 3, "v")
+        st(7, 3, 4)

@@ -144,17 +144,17 @@ def tile_liquidcell_pa_t_kernel(
                 banks[(k, c, half)] = bank
             if k == "x":
                 g = grp.tile([P, 2048], BF16, name="gx", tag="gx", bufs=3, align_bytes=64)
-                codes = qp.tile([P, 512], U32, name="xc", tag="xc", bufs=3, align_bytes=64)
-                scales = qp.tile([P, 512], U8, name="xs", tag="xs", bufs=3, align_bytes=64)
+                codes = qp.tile([P, 512], U32, name="xc", tag="xc", bufs=3, align_bytes=256)
+                scales = qp.tile([P, 512], U8, name="xs", tag="xs", bufs=3, align_bytes=256)
             elif k == "h":
                 g = grp.tile([P, 2048], BF16, name="gh", tag="gh", bufs=4, align_bytes=64)
-                codes = qp.tile([P, 512], U32, name="hc", tag="hc", bufs=3, align_bytes=64)
-                scales = qp.tile([P, 512], U8, name="hs", tag="hs", bufs=3, align_bytes=64)
+                codes = qp.tile([P, 512], U32, name="hc", tag="hc", bufs=3, align_bytes=256)
+                scales = qp.tile([P, 512], U8, name="hs", tag="hs", bufs=3, align_bytes=256)
                 g_hid[c] = g[:, 0 : 4 * n].rearrange("p (b t) -> p t b", t=4)
             else:
                 g = grp.tile([P, 2048], BF16, name="gw", tag="gw", bufs=3, align_bytes=64)
-                codes = wq.tile([P, 512], U32, name="w_codes" + k, align_bytes=64)
-                scales = wq.tile([P, 512], U8, name="w_scales" + k, align_bytes=64)
+                codes = wq.tile([P, 512], U32, name="w_codes" + k, align_bytes=256)
+                scales = wq.tile([P, 512], U8, name="w_scales" + k, align_bytes=256)
             units[(k, c)] = (g[:, 0 : 4 * n], codes[:, 0:n], scales[:, 0:n])
 
         def cp(k, c, half, engine):
@@ -275,6 +275,44 @@ def tile_liquidcell_pa_t_kernel(
                     b_banks[(c, r)][:, t, :], lhsT=v_tiles[c][:, t, r * P : (r + 1) * P],
                     rhs=ident[:], start=False, stop=(t == 3), is_transpose=True,
                 )
+
+        def prh(c, r, u):
+            cols = slice(r * P, (r + 1) * P)
+            ts = slice(2 * u, 2 * u + 2)
+            nc.vector.tensor_tensor(
+                out=v_tiles[c][:, ts, cols], in0=v_tiles[c][:, ts, cols],
+                in1=a_tiles[c][:, ts, cols], op=ALU.mult,
+            )
+
+        def bhh(c, r, u):
+            bt = psum.tile([P, 2, P], F32, name="bth", tag="ps")
+            nc.tensor.matmul(
+                bt[:].rearrange("b t p -> b (t p)"), lhsT=ident_h[:],
+                rhs=h_nat[c][:, r, u * 256 : (u + 1) * 256].rearrange("b (p e) -> b e p", e=2),
+                start=True, stop=False,
+            )
+            b_banks[(c, r, u)] = bt
+
+        def bph(c, r, u):
+            for t in range(2):
+                nc.tensor.matmul(
+                    b_banks[(c, r, u)][:, t, :],
+                    lhsT=v_tiles[c][:, 2 * u + t, r * P : (r + 1) * P],
+                    rhs=ident[:], start=False, stop=(t == 1), is_transpose=True,
+                )
+
+        def fch(c, r, u, engine):
+            copy_on(
+                engine,
+                o_tiles[c][:, r, u * 256 : (u + 1) * 256].rearrange("b (p e) -> b p e", e=2),
+                b_banks[(c, r, u)][:].rearrange("b e p -> b p e"),
+            )
+
+        def sth(c, r, u):
+            nc.sync.dma_start(
+                out=chunk_rows(out, c)[:, r, u * 256 : (u + 1) * 256],
+                in_=o_tiles[c][:, r, u * 256 : (u + 1) * 256],
+            )
 
         def o_rows(c, r):
             if c not in o_tiles:
@@ -514,7 +552,8 @@ def tile_liquidcell_pa_t_kernel(
         ms(7, 0)
         ms(7, 1)
         bk(6, 0)
-        bk(6, 1)
+        bh(6, 1)
+        bp(6, 1)
         bh(6, 2)
         bp(6, 2)
         bh(6, 3)
@@ -522,10 +561,11 @@ def tile_liquidcell_pa_t_kernel(
         wt(7, (0, 1, 2, 3,), "s")
         df(7)
         fa(6, 0)
-        fa(6, 1)
+        fc(6, 1, "s")
+        st(6, 0, 2)
         fc(6, 2, "s")
         fc(6, 3, "s")
-        st(6, 0, 4)
+        st(6, 2, 4)
         bh(7, 0)
         pr(7, 0, 1)
         bp(7, 0)
@@ -541,8 +581,13 @@ def tile_liquidcell_pa_t_kernel(
         bp(7, 2)
         fc(7, 2, "s")
         st(7, 2, 3)
-        bh(7, 3)
-        pr(7, 3, 4)
-        bp(7, 3)
-        fc(7, 3, "v")
-        st(7, 3, 4)
+        bhh(7, 3, 0)
+        prh(7, 3, 0)
+        bph(7, 3, 0)
+        bhh(7, 3, 1)
+        prh(7, 3, 1)
+        bph(7, 3, 1)
+        fch(7, 3, 0, "s")
+        fch(7, 3, 1, "v")
+        sth(7, 3, 0)
+        sth(7, 3, 1)

from contextlib import ExitStack
import math

import concourse.masks as masks
import concourse.mybir as mybir

F32 = mybir.dt.float32
BF16 = mybir.dt.bfloat16
U32 = mybir.dt.uint32
U8 = mybir.dt.uint8
FP8X4 = mybir.dt.float8_e4m3fn_x4
ALU = mybir.AluOpType
ACT = mybir.ActivationFunctionType

P = 128
B, I, H = 4096, 512, 512
CHUNKS = (512, 512, 512, 512, 512, 512, 512, 512)
N_CHUNKS = len(CHUNKS)
FLOPS = 4 * 2 * B * 512 * 512


def tile_liquidcell_pa_t_kernel(
    tc, x, hidden, W_rec, W_in_w, W_in_b, tau_base, tau_adapt_w, tau_adapt_b, out
):
    nc = tc.nc
    with ExitStack() as ctx:
        const = ctx.enter_context(tc.tile_pool(name="const", bufs=1))
        nat = ctx.enter_context(tc.tile_pool(name="nat", bufs=1))
        wq = ctx.enter_context(tc.tile_pool(name="wq", bufs=1))
        grp = ctx.enter_context(tc.tile_pool(name="grp", bufs=2))
        qp = ctx.enter_context(tc.tile_pool(name="qp", bufs=2))
        ep = ctx.enter_context(tc.tile_pool(name="ep", bufs=2))
        psum = ctx.enter_context(tc.psum_pool(name="psum", bufs=8))
        ctx.enter_context(tc.manual_schedule())

        warm = const.tile([P, 1], F32, name="warm")
        nc.vector.memset(warm[:], 0.0)
        warm2 = const.tile([P, 1], F32, name="warm2")
        nc.scalar.activation(out=warm2[:], in_=warm[:], func=ACT.Tanh)

        ident = const.tile([P, P], F32, name="ident")
        masks.make_identity(nc, ident[:])
        ident_h = const.tile([P, P], BF16, name="ident_h")
        masks.make_identity(nc, ident_h[:])

        vec_rows = const.tile([P, 256], BF16, name="vec_rows")
        nc.vector.memset(vec_rows[:], 0.0)

        def load_vectors():
            for i, vec in enumerate((W_in_b, tau_base, tau_adapt_b)):
                nc.sync.dma_start(
                    out=vec_rows[2 * i : 2 * i + 2, :],
                    in_=vec.rearrange("(u w) -> u w", u=2),
                )

        win_nat = nat.tile([P, 4, 512], BF16, name="win_nat")
        wrec_nat = nat.tile([P, 4, 512], BF16, name="wrec_nat")
        wtx_nat = nat.tile([P, 4, 512], BF16, name="wtx_nat")
        wth_nat = nat.tile([P, 4, 512], BF16, name="wth_nat")
        x_nat = []
        h_nat = []
        row0 = []
        for c, n in enumerate(CHUNKS):
            row0.append(sum(CHUNKS[0:c]))
            x_nat.append(nat.tile([P, n // P, 512], BF16, name="x_nat%d" % c))
            h_nat.append(nat.tile([P, n // P, 512], BF16, name="h_nat%d" % c))

        def chunk_rows(src, c):
            return src[row0[c] : row0[c] + CHUNKS[c], :].rearrange(
                "(p r) k -> p r k", r=CHUNKS[c] // P
            )

        def load_weight(dst, src):
            nc.sync.dma_start(
                out=dst[:].rearrange("p (u e) k -> p u e k", u=2),
                in_=src.rearrange("(u p e) k -> p u e k", u=2, e=2),
            )

        def load_tau_rows(dst, u, cols):
            nc.sync.dma_start(
                out=dst[:, 2 * u : 2 * u + 2, :],
                in_=tau_adapt_w[u * 256 : (u + 1) * 256, cols].rearrange(
                    "(p e) k -> p e k", e=2
                ),
            )

        def load_x(c):
            nc.sync.dma_start(out=x_nat[c][:], in_=chunk_rows(x, c))

        def load_h(c):
            nc.sync.dma_start(out=h_nat[c][:], in_=chunk_rows(hidden, c))

        load_weight(win_nat, W_in_w)
        load_x(0)
        load_vectors()
        load_weight(wrec_nat, W_rec)
        load_h(0)
        for u in range(2):
            load_tau_rows(wtx_nat, u, slice(0, I))
        for u in range(2):
            load_tau_rows(wth_nat, u, slice(I, I + H))
        load_x(1)
        load_h(1)
        load_x(2)
        load_h(2)
        load_x(3)
        load_h(3)
        load_x(4)
        load_h(4)
        load_x(5)
        load_h(5)
        load_x(6)
        load_h(6)
        load_x(7)
        load_h(7)

        def copy_on(engine, dst, src):
            if engine == "v":
                nc.vector.tensor_copy(out=dst, in_=src)
            else:
                nc.scalar.copy(out=dst, in_=src)

        units = {}
        ops = {}
        g_hid = {}
        banks = {}

        def tr(k, c):
            n = 512 if k in ("win", "wrec", "wtx", "wth") else CHUNKS[c]
            src = {"win": win_nat, "wrec": wrec_nat, "wtx": wtx_nat, "wth": wth_nat}.get(k)
            if k == "x":
                src = x_nat[c]
            if k == "h":
                src = h_nat[c]
            words = src[:].bitcast(F32)
            for half in range(n // 256):
                bank = psum.tile([P, 2, 256], F32, name="bank", tag="ps")
                for j in range(2):
                    for u in range(2):
                        nc.tensor.transpose(
                            bank[:, u, j * P : (j + 1) * P],
                            words[:, 2 * half + j, u * P : (u + 1) * P], ident[:],
                        )
                banks[(k, c, half)] = bank
            if k == "x":
                g = grp.tile([P, 2048], BF16, name="gx", tag="gx", bufs=3, align_bytes=64)
                codes = qp.tile([P, 512], U32, name="xc", tag="xc", bufs=3, align_bytes=256)
                scales = qp.tile([P, 512], U8, name="xs", tag="xs", bufs=3, align_bytes=256)
            elif k == "h":
                g = grp.tile([P, 2048], BF16, name="gh", tag="gh", bufs=4, align_bytes=64)
                codes = qp.tile([P, 512], U32, name="hc", tag="hc", bufs=3, align_bytes=256)
                scales = qp.tile([P, 512], U8, name="hs", tag="hs", bufs=3, align_bytes=256)
                g_hid[c] = g[:, 0 : 4 * n].rearrange("p (b t) -> p t b", t=4)
            else:
                g = grp.tile([P, 2048], BF16, name="gw", tag="gw", bufs=3, align_bytes=64)
                codes = wq.tile([P, 512], U32, name="w_codes" + k, align_bytes=256)
                scales = wq.tile([P, 512], U8, name="w_scales" + k, align_bytes=256)
            units[(k, c)] = (g[:, 0 : 4 * n], codes[:, 0:n], scales[:, 0:n])

        def cp(k, c, half, engine):
            gw = units[(k, c)][0].bitcast(F32).rearrange("p (b u) -> p b u", u=2)
            copy_on(
                engine, gw[:, half * 256 : (half + 1) * 256, :],
                banks[(k, c, half)][:].rearrange("p u b -> p b u"),
            )

        def q(k, c):
            g, codes, scales = units[(k, c)]
            nc.vector.quantize_mx(out=codes.bitcast(FP8X4), scales=scales, in_=g)

        a_tiles = {}
        v_tiles = {}
        o_tiles = {}
        accs = {}
        W = {(0, 0): "win", (0, 1): "wrec", (1, 0): "wtx", (1, 1): "wth"}

        def mp(c, o, g, t):
            cols = slice(t * P, (t + 1) * P)
            if (c, o, t) not in accs:
                acc = psum.tile([P, 512], F32, name="acc", tag="ps")
                accs[(c, o, t)] = acc
            w = units[(W[(o, g)], 0)]
            a = units[("xh"[g], c)]
            nc.tensor.matmul_mx(
                out=accs[(c, o, t)][:, 0 : CHUNKS[c]],
                lhsT=w[1][:, cols].bitcast(FP8X4), lhsT_scale=w[2][:, cols],
                rhs=a[1].bitcast(FP8X4), rhs_scale=a[2],
                start=(g == 0), stop=(g == 1),
            )

        def mg(c, o, g):
            for t in range(4):
                mp(c, o, g, t)

        def mt(c, o, t):
            mp(c, o, 0, t)
            mp(c, o, 1, t)

        def th(c, o, t):
            n = CHUNKS[c]
            tiles = (a_tiles, v_tiles)[o]
            if c not in tiles:
                if o == 0:
                    a_t = ep.tile([P, 4, 512], F32, name="a_t", tag="a_t", bufs=3)
                    tiles[c] = a_t
                else:
                    v_t = ep.tile([P, 4, 512], F32, name="v_t", tag="v_t", bufs=3)
                    tiles[c] = v_t
            nc.scalar.activation(
                out=tiles[c][:, t, 0:n], in_=accs[(c, o, t)][:, 0:n], func=ACT.Tanh,
                bias=(cst, b_tau)[o][:, t : t + 1], scale=(1.0, 0.5)[o],
            )

        def ms(c, o):
            for t in range(4):
                mt(c, o, t)
                th(c, o, t)

        def df(c):
            n = CHUNKS[c]
            nc.vector.tensor_tensor(
                out=a_tiles[c][:, :, 0:n], in0=a_tiles[c][:, :, 0:n], in1=g_hid[c], op=ALU.subtract
            )

        def wt(c, ts, engine):
            n = CHUNKS[c]
            for t in ts:
                v_cols = v_tiles[c][:, t, 0:n]
                mult, plus = neg_c[:, t : t + 1], two_c[:, t : t + 1]
                if engine == "s":
                    nc.scalar.activation(
                        out=v_cols, in_=v_cols, func=ACT.Identity, bias=plus, scale=mult
                    )
                else:
                    (nc.vector if engine == "v" else nc.gpsimd).tensor_scalar(
                        out=v_cols, in0=v_cols, scalar1=mult, scalar2=plus,
                        op0=ALU.mult, op1=ALU.add,
                    )

        def pr(c, r0, r1):
            cols = slice(r0 * P, r1 * P)
            nc.vector.tensor_tensor(
                out=v_tiles[c][:, :, cols], in0=v_tiles[c][:, :, cols],
                in1=a_tiles[c][:, :, cols], op=ALU.mult,
            )

        b_banks = {}

        def bk(c, r, pool="t"):
            if pool == "t":
                bt = psum.tile([P, 4, P], F32, name="bt", tag="ps")
            else:
                bt = psum.tile([P, 4, P], F32, name="bta", tag="ps")
            for t in range(4):
                nc.tensor.transpose(
                    bt[:, t, :], v_tiles[c][:, t, r * P : (r + 1) * P], ident[:]
                )
            b_banks[(c, r)] = bt

        def bh(c, r, pool="t"):
            if pool == "t":
                bt = psum.tile([P, 4, P], F32, name="bt", tag="ps")
            else:
                bt = psum.tile([P, 4, P], F32, name="bta", tag="ps")
            nc.tensor.matmul(
                bt[:].rearrange("b t p -> b (t p)"), lhsT=ident_h[:],
                rhs=h_nat[c][:, r, :].rearrange("b (u p e) -> b u e p", u=2, e=2),
                start=True, stop=False,
            )
            b_banks[(c, r)] = bt

        def bp(c, r):
            for t in range(4):
                nc.tensor.matmul(
                    b_banks[(c, r)][:, t, :], lhsT=v_tiles[c][:, t, r * P : (r + 1) * P],
                    rhs=ident[:], start=False, stop=(t == 3), is_transpose=True,
                )

        def prh(c, r, u):
            cols = slice(r * P, (r + 1) * P)
            ts = slice(2 * u, 2 * u + 2)
            nc.vector.tensor_tensor(
                out=v_tiles[c][:, ts, cols], in0=v_tiles[c][:, ts, cols],
                in1=a_tiles[c][:, ts, cols], op=ALU.mult,
            )

        def bhh(c, r, u):
            bt = psum.tile([P, 2, P], F32, name="bth", tag="ps")
            nc.tensor.matmul(
                bt[:].rearrange("b t p -> b (t p)"), lhsT=ident_h[:],
                rhs=h_nat[c][:, r, u * 256 : (u + 1) * 256].rearrange("b (p e) -> b e p", e=2),
                start=True, stop=False,
            )
            b_banks[(c, r, u)] = bt

        def bph(c, r, u):
            for t in range(2):
                nc.tensor.matmul(
                    b_banks[(c, r, u)][:, t, :],
                    lhsT=v_tiles[c][:, 2 * u + t, r * P : (r + 1) * P],
                    rhs=ident[:], start=False, stop=(t == 1), is_transpose=True,
                )

        def fch(c, r, u, engine):
            copy_on(
                engine,
                o_tiles[c][:, r, u * 256 : (u + 1) * 256].rearrange("b (p e) -> b p e", e=2),
                b_banks[(c, r, u)][:].rearrange("b e p -> b p e"),
            )

        def sth(c, r, u):
            nc.sync.dma_start(
                out=chunk_rows(out, c)[:, r, u * 256 : (u + 1) * 256],
                in_=o_tiles[c][:, r, u * 256 : (u + 1) * 256],
            )

        def o_rows(c, r):
            if c not in o_tiles:
                o_sb = ep.tile([P, 4, 512], F32, name="o_sb", tag="o_sb", bufs=2)
                o_tiles[c] = o_sb
            return o_tiles[c][:, r, :].rearrange("b (u p e) -> b u p e", u=2, e=2)

        def fa(c, r):
            nc.vector.tensor_tensor(
                out=o_rows(c, r),
                in0=b_banks[(c, r)][:].rearrange("b (u e) p -> b u p e", u=2),
                in1=h_nat[c][:, r, :].rearrange("b (u p e) -> b u p e", u=2, e=2),
                op=ALU.add,
            )

        def fc(c, r, engine):
            copy_on(
                engine, o_rows(c, r),
                b_banks[(c, r)][:].rearrange("b (u e) p -> b u p e", u=2),
            )

        def st(c, r0, r1):
            nc.sync.dma_start(
                out=chunk_rows(out, c)[:, r0:r1, :], in_=o_tiles[c][:, r0:r1, :]
            )

        cst = const.tile([P, 12], F32, name="cst")
        b_tau = const.tile([P, 4], F32, name="b_tau")
        inv_tb = const.tile([P, 4], F32, name="inv_tb")
        neg_c = const.tile([P, 4], F32, name="neg_c")
        two_c = const.tile([P, 4], F32, name="two_c")

        def constants():
            vt = psum.tile([P, 2, 256], F32, name="vt", tag="ps")
            nc.tensor.transpose(vt[:, 0, 0:P], vec_rows[:].bitcast(F32), ident[:])
            nc.scalar.copy(
                out=cst[:], in_=vt[:].rearrange("p u b -> p (u b)").bitcast(BF16)[:, 0:12]
            )
            nc.gpsimd.tensor_scalar(
                out=b_tau[:], in0=cst[:, 8:12], scalar1=0.5, scalar2=0.5 * math.log(3.0),
                op0=ALU.mult, op1=ALU.add,
            )

        def factors():
            nc.vector.reciprocal(out=inv_tb[:], in_=cst[:, 4:8])
            nc.gpsimd.tensor_scalar(
                out=neg_c[:], in0=inv_tb[:], scalar1=-1.0 / 15.0, scalar2=0.0,
                op0=ALU.mult, op1=ALU.add,
            )
            nc.gpsimd.tensor_scalar(
                out=two_c[:], in0=inv_tb[:], scalar1=2.0 / 15.0, scalar2=0.0,
                op0=ALU.mult, op1=ALU.add,
            )

        tr("win", 0)
        cp("win", 0, 0, "v")
        cp("win", 0, 1, "s")
        tr("x", 0)
        cp("x", 0, 0, "v")
        cp("x", 0, 1, "s")
        q("win", 0)
        q("x", 0)
        tr("wrec", 0)
        cp("wrec", 0, 0, "v")
        cp("wrec", 0, 1, "s")
        q("wrec", 0)
        tr("h", 0)
        cp("h", 0, 0, "s")
        cp("h", 0, 1, "s")
        q("h", 0)
        constants()
        mg(0, 0, 0)
        tr("wtx", 0)
        cp("wtx", 0, 0, "s")
        cp("wtx", 0, 1, "s")
        tr("wth", 0)
        cp("wth", 0, 0, "v")
        cp("wth", 0, 1, "s")
        mg(0, 0, 1)
        th(0, 0, 0)
        th(0, 0, 1)
        th(0, 0, 2)
        th(0, 0, 3)
        q("wtx", 0)
        q("wth", 0)
        factors()
        tr("x", 1)
        cp("x", 1, 0, "v")
        cp("x", 1, 1, "v")
        tr("h", 1)
        cp("h", 1, 0, "v")
        cp("h", 1, 1, "s")
        q("x", 1)
        q("h", 1)
        ms(0, 1)
        tr("x", 2)
        cp("x", 2, 0, "s")
        cp("x", 2, 1, "s")
        tr("h", 2)
        cp("h", 2, 0, "s")
        cp("h", 2, 1, "s")
        df(0)
        wt(0, (0, 1, 2, 3,), "v")
        pr(0, 0, 4)
        q("x", 2)
        q("h", 2)
        ms(1, 0)
        ms(1, 1)
        tr("x", 3)
        cp("x", 3, 0, "s")
        cp("x", 3, 1, "s")
        tr("h", 3)
        cp("h", 3, 0, "s")
        cp("h", 3, 1, "s")
        bk(0, 0)
        bk(0, 1)
        bk(0, 2)
        bk(0, 3)
        wt(1, (0, 1,), "s")
        df(1)
        wt(1, (2, 3,), "g")
        fa(0, 0)
        fa(0, 1)
        fa(0, 2)
        fa(0, 3)
        st(0, 0, 4)
        pr(1, 0, 4)
        q("x", 3)
        q("h", 3)
        ms(2, 0)
        ms(2, 1)
        tr("x", 4)
        cp("x", 4, 0, "s")
        cp("x", 4, 1, "s")
        tr("h", 4)
        cp("h", 4, 0, "s")
        cp("h", 4, 1, "s")
        bk(1, 0)
        bk(1, 1)
        bk(1, 2)
        bk(1, 3)
        wt(2, (0, 1,), "s")
        df(2)
        wt(2, (2, 3,), "g")
        fa(1, 0)
        fa(1, 1)
        fa(1, 2)
        fa(1, 3)
        st(1, 0, 4)
        pr(2, 0, 4)
        q("x", 4)
        q("h", 4)
        ms(3, 0)
        ms(3, 1)
        tr("x", 5)
        cp("x", 5, 0, "s")
        cp("x", 5, 1, "s")
        tr("h", 5)
        cp("h", 5, 0, "s")
        cp("h", 5, 1, "s")
        bk(2, 0)
        bk(2, 1)
        bk(2, 2)
        bk(2, 3)
        wt(3, (0, 1,), "s")
        df(3)
        wt(3, (2, 3,), "g")
        fa(2, 0)
        fa(2, 1)
        fa(2, 2)
        fa(2, 3)
        st(2, 0, 4)
        pr(3, 0, 4)
        q("x", 5)
        q("h", 5)
        ms(4, 0)
        ms(4, 1)
        tr("x", 6)
        cp("x", 6, 0, "s")
        cp("x", 6, 1, "s")
        tr("h", 6)
        cp("h", 6, 0, "s")
        cp("h", 6, 1, "s")
        bk(3, 0)
        bk(3, 1)
        bk(3, 2)
        bk(3, 3)
        wt(4, (0, 1,), "s")
        df(4)
        wt(4, (2, 3,), "g")
        fa(3, 0)
        fa(3, 1)
        fa(3, 2)
        fa(3, 3)
        st(3, 0, 4)
        pr(4, 0, 4)
        q("x", 6)
        q("h", 6)
        ms(5, 0)
        ms(5, 1)
        tr("x", 7)
        cp("x", 7, 0, "s")
        cp("x", 7, 1, "s")
        tr("h", 7)
        cp("h", 7, 0, "s")
        cp("h", 7, 1, "s")
        bk(4, 0)
        bk(4, 1)
        bk(4, 2)
        bk(4, 3)
        wt(5, (0, 1,), "s")
        df(5)
        wt(5, (2, 3,), "g")
        fa(4, 0)
        fa(4, 1)
        fa(4, 2)
        fa(4, 3)
        st(4, 0, 4)
        pr(5, 0, 4)
        q("x", 7)
        q("h", 7)
        ms(6, 0)
        ms(6, 1)
        bk(5, 0)
        bk(5, 1)
        bk(5, 2)
        bk(5, 3)
        wt(6, (0, 1,), "s")
        df(6)
        wt(6, (2, 3,), "g")
        fa(5, 0)
        fa(5, 1)
        fa(5, 2)
        fa(5, 3)
        st(5, 0, 4)
        pr(6, 0, 4)
        ms(7, 0)
        ms(7, 1)
        bk(6, 0)
        bh(6, 1)
        bp(6, 1)
        bh(6, 2)
        bp(6, 2)
        bh(6, 3)
        bp(6, 3)
        wt(7, (0, 1, 2, 3,), "s")
        df(7)
        fa(6, 0)
        fc(6, 1, "s")
        st(6, 0, 2)
        fc(6, 2, "s")
        fc(6, 3, "s")
        st(6, 2, 4)
        bh(7, 0)
        pr(7, 0, 1)
        bp(7, 0)
        fc(7, 0, "s")
        st(7, 0, 1)
        bh(7, 1)
        pr(7, 1, 2)
        bp(7, 1)
        fc(7, 1, "s")
        st(7, 1, 2)
        bh(7, 2)
        pr(7, 2, 3)
        bp(7, 2)
        fc(7, 2, "s")
        st(7, 2, 3)
        bhh(7, 3, 0)
        prh(7, 3, 0)
        bph(7, 3, 0)
        bhh(7, 3, 1)
        prh(7, 3, 1)
        bph(7, 3, 1)
        fch(7, 3, 0, "s")
        fch(7, 3, 1, "v")
        sth(7, 3, 0)
        sth(7, 3, 1)
